import numpy as np
import ml_dtypes


def mxq(x, axis, fmt="e4m3"):
    dtype, down = {"e4m3": (ml_dtypes.float8_e4m3fn, 7), "e5m2": (ml_dtypes.float8_e5m2, 14)}[fmt]
    v = np.moveaxis(np.asarray(x, np.float32).astype(ml_dtypes.bfloat16).astype(np.float64), axis, -1)
    blocks = v.reshape(v.shape[:-1] + (-1, 32))
    amax = np.abs(blocks).max(-1, keepdims=True)
    byte = np.maximum(np.where(amax > 0, np.frexp(amax)[1] - 1 + 127, 0) - down, 1)
    scale = np.exp2(byte - 127.0)
    codes = (blocks / scale).astype(np.float32).astype(dtype).astype(np.float64)
    return np.moveaxis((codes * scale).reshape(v.shape), -1, axis)


WIDE = False


def mx_kscale(k):
    if not WIDE:
        return np.ones(k)
    levels = np.array([10, -10, 5, -5, 0])
    if k % 512:
        return np.exp2(np.random.permutation(np.resize(levels, k // 32))).repeat(32)
    a = np.empty((k // 512, 16))
    for p in range(k // 512):
        a[p, :8] = np.random.permutation(np.resize(levels, 8))
        for g in range(8):
            far = levels[np.abs(levels - a[p, g]) >= 10]
            a[p, g + 8] = far[np.random.randint(len(far))]
    return np.exp2(a.ravel()).repeat(32)


BF16 = ml_dtypes.bfloat16


def bf(x):
    return np.asarray(x, np.float32).astype(BF16)


def f64(x):
    return np.asarray(x).astype(np.float64)


A, L, B, V, D = 128, 32, 128, 16, 512
TAU = 100.0
EPS = 1e-6


def _norm(a):
    n = np.sqrt(np.sum(a * a, axis=-1, keepdims=True))
    return a / np.maximum(n, EPS)


def softmax(z, axis):
    e = np.exp(z - z.max(axis=axis, keepdims=True))
    return e / e.sum(axis=axis, keepdims=True)


def setup_inputs():
    s = mx_kscale(D)
    lens = np.random.randint(L // 2, L + 1, size=A)
    mask = (np.arange(L)[None, :] < lens[:, None]).astype(np.float64)
    c = 2.0 ** np.round(0.5 * np.log2(np.mean(s * s) * np.mean(1.0 / (s * s))))
    return {"text_feat": bf(np.random.standard_normal((A, L, D)) * s), "video_feat": bf(np.random.standard_normal((B, V, D)) / s), "text_mask": bf(mask * c)}


def reference(text_feat, video_feat, text_mask):
    tf = _norm(f64(text_feat))
    vf = _norm(f64(video_feat))
    tq = mxq(tf, 2, "e4m3").reshape(A * L, D)
    vq = mxq(vf, 2, "e4m3").reshape(B * V, D)
    r = (tq @ vq.T).reshape(A, L, B, V).transpose(0, 2, 1, 3)
    r = r * f64(text_mask)[:, None, :, None]
    ps1 = softmax(r * TAU, -1)
    t2v = np.sum(r * ps1, axis=-1)
    ps2 = softmax(np.where(r == 0, -np.inf, r) * TAU, -2)
    v2t = np.sum(r * ps2, axis=-2)
    ps3 = softmax(np.where(t2v == 0, -np.inf, t2v) * TAU, -1)
    t2v_ab = np.sum(t2v * ps3, axis=2)
    ps4 = softmax(v2t * TAU, -1)
    v2t_ab = np.sum(v2t * ps4, axis=2)
    return (t2v_ab + v2t_ab) / 2.0

@@ -1,0 +1,552 @@
+from contextlib import ExitStack
+
+import concourse.mybir as mybir
+from concourse.masks import make_identity
+
+F32 = mybir.dt.float32
+BF16 = mybir.dt.bfloat16
+U32 = mybir.dt.uint32
+U8 = mybir.dt.uint8
+FP8X4 = mybir.dt.float8_e4m3fn_x4
+ALU = mybir.AluOpType
+FN = mybir.ActivationFunctionType
+INNERMOST = mybir.AxisListType.X
+
+P = 128
+TOKENS = 32
+FRAMES = 16
+FEATURES = 512
+PACK = 4
+TAU = 100.0
+EPS = 1.0e-6
+BARRED = -1.0e30
+
+GROUPS = 4
+GROUP_VIDEOS = P // GROUPS
+GROUP_COLS = FRAMES * GROUP_VIDEOS
+BLOCKS = GROUP_COLS // P
+QUAD = 4
+QUADS = TOKENS // QUAD
+FRAME_SUM_COLS = QUADS * P
+PHASE_SUM_COLS = GROUP_COLS + FRAME_SUM_COLS
+SUM_COLS = GROUPS * PHASE_SUM_COLS
+
+FIRST_STEPS = GROUPS * TOKENS
+STEPS = FIRST_STEPS + TOKENS
+FIRST_SWEEP_PASSES = 2
+PAIR = 2
+SUM_LAG = 4
+PIECES_PER_STEP = 2
+
+FLOPS = 2 * (P * TOKENS) * (P * FRAMES) * FEATURES
+
+
+def tile_mug_head_kernel(tc, text_feat, video_feat, text_mask, out):
+    nc = tc.nc
+    with ExitStack() as pools:
+        consts = pools.enter_context(tc.tile_pool(name="consts", bufs=1))
+        keep = pools.enter_context(tc.tile_pool(name="keep", bufs=1))
+        psum = pools.enter_context(tc.psum_pool(name="psum", bufs=2))
+
+        ident_f32 = consts.tile([P, P], F32, name="ident_f32")
+        make_identity(nc, ident_f32[:])
+        ident_bf16 = consts.tile([P, P], BF16, name="ident_bf16")
+        make_identity(nc, ident_bf16[:])
+
+        mask_bf16 = consts.tile([P, TOKENS], BF16, name="mask_bf16")
+        nc.sync.dma_start(out=mask_bf16[:], in_=text_mask)
+        mask = consts.tile([P, TOKENS], F32, name="mask")
+        nc.vector.tensor_copy(out=mask[:], in_=mask_bf16[:])
+        sharp_mask = consts.tile([P, TOKENS], F32, name="sharp_mask")
+        nc.vector.tensor_scalar_mul(out=sharp_mask[:], in0=mask[:], scalar1=TAU)
+        barred = consts.tile([P, TOKENS], F32, name="barred")
+        nc.vector.tensor_scalar(
+            out=barred[:], in0=mask[:], scalar1=0.0, scalar2=BARRED, op0=ALU.is_equal, op1=ALU.mult
+        )
+        mask_top = consts.tile([P, 1], F32, name="mask_top")
+        nc.vector.tensor_reduce(out=mask_top[:], in_=mask[:], axis=INNERMOST, op=ALU.max)
+
+        text_codes = keep.tile([P, TOKENS * P], U32, name="text_codes", align_bytes=64)
+        text_scales = keep.tile([P, TOKENS * P], U8, name="text_scales", align_bytes=64)
+        video_codes = keep.tile([P, GROUPS * GROUP_COLS], U32, name="video_codes", align_bytes=64)
+        video_scales = keep.tile([P, GROUPS * GROUP_COLS], U8, name="video_scales", align_bytes=64)
+        frame_top = keep.tile([P, GROUPS, TOKENS, GROUP_VIDEOS], F32, name="frame_top")
+        token_top = keep.tile([P, GROUPS, GROUP_COLS], F32, name="token_top")
+        sums = keep.tile([P, 2, SUM_COLS], F32, name="sums")
+
+        def transpose_add(acc, block, start, stop):
+            nc.tensor.matmul(
+                out=acc, lhsT=block, rhs=ident_f32[:], is_transpose=True, start=start, stop=stop
+            )
+
+        def inverse_norms(pool, raw, count):
+            by_scalar = pool.tile([P, count // 2], F32, name="squares_by_scalar", bufs=1)
+            by_vector = pool.tile([P, count // 2], F32, name="squares_by_vector", bufs=1)
+            for i in range(count):
+                total = slice(i // 2, i // 2 + 1)
+                if i % 2 == 0:
+                    squares = pool.tile([P, FEATURES], BF16, tag="squares_s", name="squares_s")
+                    nc.scalar.activation(
+                        out=squares[:], in_=raw[:, i, :], func=FN.Square, accum_out=by_scalar[:, total]
+                    )
+                else:
+                    squares = pool.tile([P, FEATURES], F32, tag="squares_v", name="squares_v")
+                    nc.vector.scalar_tensor_tensor(
+                        out=squares[:], in0=raw[:, i, :], scalar=1.0, in1=raw[:, i, :],
+                        op0=ALU.mult, op1=ALU.mult, accum_out=by_vector[:, total],
+                    )
+            inverse = pool.tile([P, 2, count // 2], F32, name="inverse", bufs=1)
+            for parity, square_sum in enumerate((by_scalar, by_vector)):
+                nc.vector.tensor_scalar_max(out=square_sum[:], in0=square_sum[:], scalar1=EPS * EPS)
+                nc.scalar.sqrt(out=inverse[:, parity, :], in_=square_sum[:])
+                nc.vector.reciprocal(out=inverse[:, parity, :], in_=inverse[:, parity, :])
+            return inverse
+
+        def features_to_partitions(rows):
+            bank = psum.tile([P, PACK, P], BF16, tag="second", name="turned_rows")
+            for j in range(PACK):
+                nc.tensor.transpose(bank[:, j, :], rows[:, j * P : (j + 1) * P], ident_bf16[:])
+            return bank
+
+        with tc.tile_pool(name="video_prep", bufs=2) as video_prep:
+            video_raw = video_prep.tile([P, FRAMES, FEATURES], BF16, name="video_raw", bufs=1)
+            for first in range(0, FRAMES, 4):
+                nc.sync.dma_start(
+                    out=video_raw[:, first : first + 4, :], in_=video_feat[:, first : first + 4, :]
+                )
+            warm = video_prep.tile([P, 1], F32, name="warm", bufs=1)
+            nc.vector.memset(warm[:], 1.0)
+            nc.scalar.sqrt(out=warm[:], in_=warm[:])
+            video_inverse = inverse_norms(video_prep, video_raw, FRAMES)
+            video_grouped = video_prep.tile(
+                [P, GROUPS, FRAMES, GROUP_VIDEOS, PACK], BF16,
+                name="video_grouped", bufs=1, align_bytes=64,
+            )
+            for v in range(FRAMES):
+                rows = video_prep.tile([P, FEATURES], BF16, tag="rows", name="rows", bufs=3)
+                nc.vector.tensor_scalar_mul(
+                    out=rows[:].rearrange("b (j p) -> b j p", j=PACK),
+                    in0=video_raw[:, v, :].rearrange("b (p j) -> b j p", j=PACK),
+                    scalar1=video_inverse[:, v % 2, v // 2 : v // 2 + 1],
+                )
+                bank = features_to_partitions(rows)
+                copy = nc.scalar.copy if v % 2 == 0 else nc.vector.tensor_copy
+                copy(
+                    out=video_grouped[:, :, v, :, :],
+                    in_=bank[:].rearrange("p j (g b) -> p g b j", g=GROUPS),
+                )
+            for group in range(GROUPS):
+                cols = slice(group * GROUP_COLS, (group + 1) * GROUP_COLS)
+                nc.vector.quantize_mx(
+                    out=video_codes[:, cols].bitcast(FP8X4),
+                    scales=video_scales[:, cols],
+                    in_=video_grouped[:, group, :, :, :].rearrange("p v b j -> p (v b j)"),
+                )
+
+        quad_work = pools.enter_context(tc.tile_pool(name="quad_work", bufs=3))
+        pair_work = pools.enter_context(tc.tile_pool(name="pair_work", bufs=3))
+
+        def similarities(token, group, tag, times):
+            sim = psum.tile([P, GROUP_COLS], F32, tag=tag, name="sim")
+            texts = slice(token * P, (token + 1) * P)
+            cols = slice(group * GROUP_COLS, (group + 1) * GROUP_COLS)
+            for repeat in range(times):
+                nc.tensor.matmul_mx(
+                    out=sim[:],
+                    lhsT=text_codes[:, texts].bitcast(FP8X4),
+                    lhsT_scale=text_scales[:, texts],
+                    rhs=video_codes[:, cols].bitcast(FP8X4),
+                    rhs_scale=video_scales[:, cols],
+                    start=True,
+                    stop=True,
+                )
+            return sim
+
+        sim_first = {}
+        sim_second = {}
+        frame_tiles = {}
+        token_tiles = {}
+        quad_banks = {}
+        group_banks = {}
+
+        def frame_sum_col(group):
+            return group * PHASE_SUM_COLS
+
+        def token_sum_col(group):
+            return (group + 1) * PHASE_SUM_COLS - GROUP_COLS
+
+        def in_first_sweep(step):
+            return 0 <= step < FIRST_STEPS
+
+        def in_second_sweep(step):
+            return TOKENS <= step < STEPS
+
+        def multiply(step):
+            token = step % TOKENS
+            if in_first_sweep(step):
+                sim_first[step] = similarities(token, step // TOKENS, "first", FIRST_SWEEP_PASSES)
+            if in_second_sweep(step):
+                sim_second[step] = similarities(token, step // TOKENS - 1, "second", 1)
+
+        def subtract_tops(step):
+            token = step % TOKENS
+            group = step // TOKENS
+            top_f = None
+            if in_first_sweep(step):
+                top_f = frame_top[:, group, token, :]
+                nc.vector.tensor_reduce(
+                    out=top_f,
+                    in_=sim_first[step][:].rearrange("a (v b) -> a b v", v=FRAMES),
+                    axis=INNERMOST,
+                    op=ALU.max,
+                )
+            if in_second_sweep(step):
+                if step % PAIR == 0:
+                    pair_shape = [P, PAIR, GROUP_COLS]
+                    token_tiles[step // PAIR] = (
+                        pair_work.tile(pair_shape, F32, tag="dev_t", name="dev_t"),
+                        pair_work.tile(pair_shape, F32, tag="wgt_t", name="wgt_t"),
+                    )
+                nc.vector.scalar_tensor_tensor(
+                    out=token_tiles[step // PAIR][0][:, step % PAIR, :],
+                    in0=sim_second[step][:],
+                    scalar=mask[:, token : token + 1],
+                    in1=token_top[:, group - 1, :],
+                    op0=ALU.mult,
+                    op1=ALU.subtract,
+                )
+            if in_first_sweep(step):
+                sim = sim_first[step]
+                if step % QUAD == 0:
+                    quad_shape = [P, FRAMES, QUAD, GROUP_VIDEOS]
+                    frame_tiles[step // QUAD] = (
+                        quad_work.tile(quad_shape, F32, tag="dev_f", name="dev_f"),
+                        quad_work.tile(quad_shape, F32, tag="wgt_f", name="wgt_f"),
+                    )
+                nc.vector.tensor_tensor(
+                    out=frame_tiles[step // QUAD][0][:, :, step % QUAD, :],
+                    in0=sim[:].rearrange("a (v b) -> a v b", v=FRAMES),
+                    in1=top_f.unsqueeze(1).to_broadcast([P, FRAMES, GROUP_VIDEOS]),
+                    op=ALU.subtract,
+                )
+                bar = barred[:, token : token + 1]
+                top_t = token_top[:, group, :]
+                if token == 0:
+                    nc.vector.tensor_scalar(
+                        out=top_t, in0=sim[:], scalar1=bar, scalar2=None, op0=ALU.add
+                    )
+                else:
+                    nc.vector.scalar_tensor_tensor(
+                        out=top_t, in0=sim[:], scalar=bar, in1=top_t, op0=ALU.add, op1=ALU.max
+                    )
+                if token == TOKENS - 1:
+                    nc.vector.tensor_scalar_mul(out=top_t, in0=top_t, scalar1=mask_top[:, 0:1])
+
+        def weigh(step):
+            token = step % TOKENS
+            if in_second_sweep(step):
+                dev_t, wgt_t = token_tiles[step // PAIR]
+                nc.scalar.activation(
+                    out=wgt_t[:, step % PAIR, :],
+                    in_=dev_t[:, step % PAIR, :],
+                    func=FN.Exp,
+                    scale=TAU,
+                    bias=barred[:, token : token + 1],
+                )
+            if in_first_sweep(step):
+                dev_f, wgt_f = frame_tiles[step // QUAD]
+                nc.scalar.activation(
+                    out=wgt_f[:, :, step % QUAD, :],
+                    in_=dev_f[:, :, step % QUAD, :],
+                    func=FN.Exp,
+                    scale=sharp_mask[:, token : token + 1],
+                )
+
+        def form_products(step):
+            if step % PAIR != PAIR - 1:
+                return
+            if in_second_sweep(step):
+                dev_t, wgt_t = token_tiles[step // PAIR]
+                nc.gpsimd.tensor_tensor(out=dev_t[:], in0=dev_t[:], in1=wgt_t[:], op=ALU.mult)
+            if in_first_sweep(step):
+                dev_f, wgt_f = frame_tiles[step // QUAD]
+                slots = slice(step % QUAD - (PAIR - 1), step % QUAD + 1)
+                nc.gpsimd.tensor_tensor(
+                    out=dev_f[:, :, slots, :],
+                    in0=dev_f[:, :, slots, :],
+                    in1=wgt_f[:, :, slots, :],
+                    op=ALU.mult,
+                )
+
+        def add_up_tokens(step):
+            if not in_second_sweep(step):
+                return
+            token = step % TOKENS
+            group = step // TOKENS - 1
+            if token == 0:
+                group_banks[group] = (
+                    psum.tile([P, GROUP_COLS], F32, tag="weight_sums", name="weight_sums", bufs=1),
+                    psum.tile([P, GROUP_COLS], F32, tag="product_sums", name="product_sums", bufs=1),
+                )
+            dev_t, wgt_t = token_tiles[step // PAIR]
+            for plane, terms in enumerate((wgt_t, dev_t)):
+                acc = group_banks[group][plane]
+                for k in range(BLOCKS):
+                    cols = slice(k * P, (k + 1) * P)
+                    transpose_add(
+                        acc[:, cols],
+                        terms[:, step % PAIR, cols],
+                        token == 0 and k == 0,
+                        token == TOKENS - 1 and k == BLOCKS - 1,
+                    )
+                if token == TOKENS - 1:
+                    first_col = token_sum_col(group)
+                    nc.scalar.copy(out=sums[:, plane, first_col : first_col + GROUP_COLS], in_=acc[:])
+
+        def add_up_frames(step):
+            if not in_first_sweep(step):
+                return
+            quad = step // QUAD
+            plane = (step % QUAD) // 2
+            first_frame = (step % 2) * (FRAMES // 2)
+            if step % QUAD == 0:
+                quad_banks[quad] = psum.tile([P, 2, P], F32, tag="quad_sums", name="quad_sums")
+            terms = frame_tiles[quad][1 - plane]
+            for v in range(first_frame, first_frame + FRAMES // 2):
+                transpose_add(
+                    quad_banks[quad][:, plane, :],
+                    terms[:, v, :, :].rearrange("a s b -> a (s b)"),
+                    v == 0,
+                    v == FRAMES - 1,
+                )
+
+        def store_frame_sums(step):
+            if in_first_sweep(step) and step % QUAD == QUAD - 1:
+                first_col = frame_sum_col(step // TOKENS) + (step % TOKENS) // QUAD * P
+                nc.scalar.copy(
+                    out=sums[:, :, first_col : first_col + P], in_=quad_banks[step // QUAD][:]
+                )
+
+        def pipeline_step(step):
+            multiply(step + 1)
+            subtract_tops(step)
+            weigh(step)
+            form_products(step - 1)
+            add_up_tokens(step - SUM_LAG)
+            add_up_frames(step - SUM_LAG)
+            store_frame_sums(step - SUM_LAG - 1)
+
+        with tc.tile_pool(name="text_prep", bufs=2) as text_prep:
+            text_raw = text_prep.tile([P, TOKENS, FEATURES], BF16, name="text_raw", bufs=1)
+            for first in range(0, TOKENS, 8):
+                nc.sync.dma_start(
+                    out=text_raw[:, first : first + 8, :], in_=text_feat[:, first : first + 8, :]
+                )
+            text_inverse = inverse_norms(text_prep, text_raw, TOKENS)
+
+            def prepare_text_quad(quad):
+                grouped = text_prep.tile(
+                    [P, QUAD, P, PACK], BF16, tag="text_grouped", name="text_grouped", align_bytes=64
+                )
+                for slot in range(QUAD):
+                    token = quad * QUAD + slot
+                    rows = text_prep.tile([P, FEATURES], BF16, tag="rows", name="rows", bufs=3)
+                    nc.scalar.activation(
+                        out=rows[:].rearrange("a (j p) -> a j p", j=PACK),
+                        in_=text_raw[:, token, :].rearrange("a (p j) -> a j p", j=PACK),
+                        func=FN.Copy,
+                        scale=text_inverse[:, token % 2, token // 2 : token // 2 + 1],
+                    )
+                    bank = features_to_partitions(rows)
+                    nc.scalar.copy(
+                        out=grouped[:, slot, :, :], in_=bank[:].rearrange("p j a -> p a j")
+                    )
+                cols = slice(quad * QUAD * P, (quad + 1) * QUAD * P)
+                nc.vector.quantize_mx(
+                    out=text_codes[:, cols].bitcast(FP8X4),
+                    scales=text_scales[:, cols],
+                    in_=grouped[:].rearrange("p s a j -> p (s a j)"),
+                )
+
+            prepare_text_quad(0)
+            for step in range(-1, TOKENS - 1):
+                if (step + 1) % QUAD == 0 and step + 1 + QUAD < TOKENS:
+                    prepare_text_quad((step + 1) // QUAD + 1)
+                pipeline_step(step)
+
+        with tc.manual_schedule():
+            for step in range(TOKENS - 1, FIRST_STEPS - 1):
+                pipeline_step(step)
+
+        finish = pools.enter_context(tc.tile_pool(name="finish", bufs=2))
+
+        def turn_back(made, first_col):
+            made["bank"] = psum.tile([P, BLOCKS * P], F32, tag="first", name="turned_back")
+            for k in range(BLOCKS):
+                block = sums[:, 1, first_col + k * P : first_col + (k + 1) * P]
+                nc.tensor.transpose(made["bank"][:, k * P : (k + 1) * P], block, ident_f32[:])
+
+        def division_pieces(first_col, last_col):
+            weights = sums[:, 0, first_col:last_col]
+
+            def invert():
+                nc.scalar.activation(out=weights, in_=weights, func=FN.Ln)
+                nc.scalar.activation(out=weights, in_=weights, func=FN.Exp, scale=-1.0)
+
+            def multiply_by_inverse(col):
+                cols = slice(col, col + GROUP_COLS)
+                nc.gpsimd.tensor_tensor(
+                    out=sums[:, 1, cols], in0=sums[:, 1, cols], in1=sums[:, 0, cols], op=ALU.mult
+                )
+
+            pieces = [invert]
+            for col in range(first_col, last_col, GROUP_COLS):
+                pieces.append(lambda col=col: multiply_by_inverse(col))
+            return pieces
+
+        def new_statistics(name):
+            return {
+                "top": finish.tile([P, P], F32, name=name + "_top", bufs=1),
+                "weights": finish.tile([P, P], F32, name=name + "_weights", bufs=1),
+                "products": finish.tile([P, P], F32, name=name + "_products", bufs=1),
+            }
+
+        def pooling_pieces(made, count, group, statistics):
+            shape = [P, GROUP_VIDEOS, count]
+            videos = slice(group * GROUP_VIDEOS, (group + 1) * GROUP_VIDEOS)
+            top = statistics["top"][:, videos]
+
+            def find_top():
+                nc.vector.tensor_reduce(out=top, in_=made["values"][:], axis=INNERMOST, op=ALU.max)
+
+            def weigh_deviations():
+                made["dev"] = finish.tile(shape, F32, tag="dev%d" % count, name="dev")
+                made["wgt"] = finish.tile(shape, F32, tag="wgt%d" % count, name="wgt")
+                nc.vector.tensor_tensor(
+                    out=made["dev"][:],
+                    in0=made["values"][:],
+                    in1=top.unsqueeze(2).to_broadcast(shape),
+                    op=ALU.subtract,
+                )
+                nc.scalar.activation(out=made["wgt"][:], in_=made["dev"][:], func=FN.Exp, scale=TAU)
+
+            def form_product():
+                nc.gpsimd.tensor_tensor(
+                    out=made["dev"][:], in0=made["dev"][:], in1=made["wgt"][:], op=ALU.mult
+                )
+
+            def add_weights():
+                nc.vector.tensor_reduce(
+                    out=statistics["weights"][:, videos], in_=made["wgt"][:],
+                    axis=INNERMOST, op=ALU.add,
+                )
+
+            def add_products():
+                nc.vector.tensor_reduce(
+                    out=statistics["products"][:, videos], in_=made["dev"][:],
+                    axis=INNERMOST, op=ALU.add,
+                )
+
+            return [find_top, weigh_deviations, form_product, add_weights, add_products]
+
+        def pooled_mean(statistics):
+            nc.vector.reciprocal(out=statistics["weights"][:], in_=statistics["weights"][:])
+            nc.vector.tensor_tensor(
+                out=statistics["products"][:], in0=statistics["products"][:],
+                in1=statistics["weights"][:], op=ALU.mult,
+            )
+            nc.vector.tensor_tensor(
+                out=statistics["products"][:], in0=statistics["products"][:],
+                in1=statistics["top"][:], op=ALU.add,
+            )
+            return statistics["products"]
+
+        def text_to_video_pieces(group, statistics):
+            made = {}
+            tokens_of_bank = BLOCKS * QUAD
+
+            def add_frame_top(first):
+                if first == 0:
+                    made["raw"] = finish.tile(
+                        [P, TOKENS, GROUP_VIDEOS], F32, tag="t2v_raw", name="t2v_raw"
+                    )
+                tokens = slice(first, first + tokens_of_bank)
+                nc.vector.tensor_tensor(
+                    out=made["raw"][:, tokens, :],
+                    in0=made["bank"][:].rearrange("a (t b) -> a t b", b=GROUP_VIDEOS),
+                    in1=frame_top[:, group, tokens, :],
+                    op=ALU.add,
+                )
+
+            def mask_and_bar():
+                made["values"] = finish.tile([P, GROUP_VIDEOS, TOKENS], F32, tag="t2v", name="t2v")
+                for token in range(TOKENS):
+                    nc.scalar.activation(
+                        out=made["values"][:, :, token],
+                        in_=made["raw"][:, token, :],
+                        func=FN.Identity,
+                        scale=mask[:, token : token + 1],
+                        bias=barred[:, token : token + 1],
+                    )
+
+            pieces = []
+            for first in range(0, TOKENS, tokens_of_bank):
+                first_col = frame_sum_col(group) + first // QUAD * P
+                pieces.append(lambda first_col=first_col: turn_back(made, first_col))
+                pieces.append(lambda first=first: add_frame_top(first))
+            pieces.append(mask_and_bar)
+            pieces.extend(pooling_pieces(made, TOKENS, group, statistics))
+            return pieces
+
+        def video_to_text_pieces(group, statistics):
+            made = {}
+
+            def add_token_top():
+                made["values"] = finish.tile([P, GROUP_VIDEOS, FRAMES], F32, tag="v2t", name="v2t")
+                nc.vector.tensor_tensor(
+                    out=made["values"][:],
+                    in0=made["bank"][:].rearrange("a (v b) -> a b v", v=FRAMES),
+                    in1=token_top[:, group, :].rearrange("a (v b) -> a b v", v=FRAMES),
+                    op=ALU.add,
+                )
+
+            pieces = [lambda: turn_back(made, token_sum_col(group)), add_token_top]
+            pieces.extend(pooling_pieces(made, FRAMES, group, statistics))
+            return pieces
+
+        over_tokens = new_statistics("over_tokens")
+        over_frames = new_statistics("over_frames")
+        last_phase_col = token_sum_col(GROUPS - 2)
+        waiting = []
+        for piece in division_pieces(0, last_phase_col):
+            waiting.append((FIRST_STEPS - 1, piece))
+        for phase in range(GROUPS + 1):
+            ready = max(FIRST_STEPS - 1, (phase + 1) * TOKENS + SUM_LAG)
+            pieces = []
+            if phase == GROUPS - 1:
+                pieces.extend(division_pieces(last_phase_col, token_sum_col(GROUPS - 1)))
+            if phase == GROUPS:
+                pieces.extend(division_pieces(token_sum_col(GROUPS - 1), SUM_COLS))
+            if phase < GROUPS:
+                pieces.extend(text_to_video_pieces(phase, over_tokens))
+            if phase > 0:
+                pieces.extend(video_to_text_pieces(phase - 1, over_frames))
+            for piece in pieces:
+                waiting.append((ready, piece))
+
+        served = 0
+        for step in range(FIRST_STEPS - 1, STEPS + SUM_LAG + 1):
+            pipeline_step(step)
+            for turn in range(PIECES_PER_STEP):
+                if served < len(waiting) and waiting[served][0] <= step:
+                    waiting[served][1]()
+                    served += 1
+        for ready, piece in waiting[served:]:
+            piece()
+
+        result = finish.tile([P, P], F32, name="result", bufs=1)
+        nc.vector.tensor_tensor(
+            out=result[:], in0=pooled_mean(over_tokens)[:], in1=pooled_mean(over_frames)[:], op=ALU.add
+        )
+        nc.vector.tensor_scalar_mul(out=result[:], in0=result[:], scalar1=0.5)
+        nc.sync.dma_start(out=out, in_=result[:])

@@ -20,22 +20,20 @@ PACK = 4
 TAU = 100.0
 EPS = 1.0e-6
 BARRED = -1.0e30
+TINY = 1.0e-30
+LOW = -1.0e-20
 
 GROUPS = 4
 GROUP_VIDEOS = P // GROUPS
 GROUP_COLS = FRAMES * GROUP_VIDEOS
 BLOCKS = GROUP_COLS // P
 QUAD = 4
-QUADS = TOKENS // QUAD
-FRAME_SUM_COLS = QUADS * P
-PHASE_SUM_COLS = GROUP_COLS + FRAME_SUM_COLS
-SUM_COLS = GROUPS * PHASE_SUM_COLS
+HALF = QUAD * BLOCKS
 
 FIRST_STEPS = GROUPS * TOKENS
 STEPS = FIRST_STEPS + TOKENS
-FIRST_SWEEP_PASSES = 2
-PAIR = 2
-SUM_LAG = 4
+FRAME_LAG = 4
+TOKEN_LAG = 2
 PIECES_PER_STEP = 2
 
 FLOPS = 2 * (P * TOKENS) * (P * FRAMES) * FEATURES
@@ -65,14 +63,22 @@ def tile_mug_head_kernel(tc, text_feat, video_feat, text_mask, out):
         )
         mask_top = consts.tile([P, 1], F32, name="mask_top")
         nc.vector.tensor_reduce(out=mask_top[:], in_=mask[:], axis=INNERMOST, op=ALU.max)
+        sharp_top = consts.tile([P, 1], F32, name="sharp_top")
+        nc.vector.tensor_scalar_mul(out=sharp_top[:], in0=mask_top[:], scalar1=TAU)
+        nudge = consts.tile([P, 2], F32, name="nudge")
+        for plane, value in enumerate((TINY, LOW)):
+            nc.vector.tensor_scalar(
+                out=nudge[:, plane : plane + 1], in0=mask_top[:], scalar1=0.0, scalar2=value,
+                op0=ALU.mult, op1=ALU.add,
+            )
 
         text_codes = keep.tile([P, TOKENS * P], U32, name="text_codes", align_bytes=64)
         text_scales = keep.tile([P, TOKENS * P], U8, name="text_scales", align_bytes=64)
         video_codes = keep.tile([P, GROUPS * GROUP_COLS], U32, name="video_codes", align_bytes=64)
         video_scales = keep.tile([P, GROUPS * GROUP_COLS], U8, name="video_scales", align_bytes=64)
-        frame_top = keep.tile([P, GROUPS, TOKENS, GROUP_VIDEOS], F32, name="frame_top")
-        token_top = keep.tile([P, GROUPS, GROUP_COLS], F32, name="token_top")
-        sums = keep.tile([P, 2, SUM_COLS], F32, name="sums")
+        top = keep.tile([P, P], F32, name="top")
+        top_turned = keep.tile([P, GROUPS, P], F32, name="top_turned")
+        statistics = keep.tile([P, 3, 2, P], F32, name="statistics")
 
         def transpose_add(acc, block, start, stop):
             nc.tensor.matmul(
@@ -103,7 +109,7 @@ def tile_mug_head_kernel(tc, text_feat, video_feat, text_mask, out):
             return inverse
 
         def features_to_partitions(rows):
-            bank = psum.tile([P, PACK, P], BF16, tag="second", name="turned_rows")
+            bank = psum.tile([P, PACK, P], BF16, tag="second", name="turned_rows", bufs=3)
             for j in range(PACK):
                 nc.tensor.transpose(bank[:, j, :], rows[:, j * P : (j + 1) * P], ident_bf16[:])
             return bank
@@ -144,10 +150,11 @@ def tile_mug_head_kernel(tc, text_feat, video_feat, text_mask, out):
                 )
 
         quad_work = pools.enter_context(tc.tile_pool(name="quad_work", bufs=3))
-        pair_work = pools.enter_context(tc.tile_pool(name="pair_work", bufs=3))
+        token_work = pools.enter_context(tc.tile_pool(name="token_work", bufs=4))
+        group_work = pools.enter_context(tc.tile_pool(name="group_work", bufs=2))
 
-        def similarities(token, group, tag, times):
-            sim = psum.tile([P, GROUP_COLS], F32, tag=tag, name="sim")
+        def similarities(token, group, tag, bufs, times):
+            sim = psum.tile([P, GROUP_COLS], F32, tag=tag, name="sim", bufs=bufs)
             texts = slice(token * P, (token + 1) * P)
             cols = slice(group * GROUP_COLS, (group + 1) * GROUP_COLS)
             for repeat in range(times):
@@ -164,16 +171,15 @@ def tile_mug_head_kernel(tc, text_feat, video_feat, text_mask, out):
 
         sim_first = {}
         sim_second = {}
-        frame_tiles = {}
-        token_tiles = {}
+        running_top = {}
+        deviations = {}
+        weights = {}
+        quad_tiles = {}
+        product_sums = {}
         quad_banks = {}
-        group_banks = {}
-
-        def frame_sum_col(group):
-            return group * PHASE_SUM_COLS
-
-        def token_sum_col(group):
-            return (group + 1) * PHASE_SUM_COLS - GROUP_COLS
+        weight_banks = {}
+        frame_sums = {}
+        token_sums = {}
 
         def in_first_sweep(step):
             return 0 <= step < FIRST_STEPS
@@ -181,160 +187,176 @@ def tile_mug_head_kernel(tc, text_feat, video_feat, text_mask, out):
         def in_second_sweep(step):
             return TOKENS <= step < STEPS
 
+        def group_videos(group):
+            return slice(group * GROUP_VIDEOS, (group + 1) * GROUP_VIDEOS)
+
         def multiply(step):
             token = step % TOKENS
-            if in_first_sweep(step):
-                sim_first[step] = similarities(token, step // TOKENS, "first", FIRST_SWEEP_PASSES)
             if in_second_sweep(step):
-                sim_second[step] = similarities(token, step // TOKENS - 1, "second", 1)
+                times = 1 if in_first_sweep(step) else 2
+                sim_second[step] = similarities(token, step // TOKENS - 1, "second", 3, times)
+            if in_first_sweep(step):
+                sim_first[step] = similarities(token, step // TOKENS, "first", 2, 1)
 
-        def subtract_tops(step):
+        def subtract_top(step):
+            if not in_second_sweep(step):
+                return
+            group = step // TOKENS - 1
+            deviations[step] = token_work.tile([P, GROUP_COLS], F32, tag="deviation", name="deviation")
+            nc.vector.tensor_tensor(
+                out=deviations[step][:].rearrange("a (v b) -> a v b", v=FRAMES),
+                in0=sim_second[step][:].rearrange("a (v b) -> a v b", v=FRAMES),
+                in1=top[:, group_videos(group)].unsqueeze(1).to_broadcast([P, FRAMES, GROUP_VIDEOS]),
+                op=ALU.subtract,
+            )
+
+        def raise_top(step):
+            if not in_first_sweep(step):
+                return
             token = step % TOKENS
             group = step // TOKENS
-            top_f = None
-            if in_first_sweep(step):
-                top_f = frame_top[:, group, token, :]
+            bar = barred[:, token : token + 1]
+            if token == 0:
+                running_top[group] = group_work.tile([P, GROUP_COLS], F32, tag="running", name="running")
+                nc.vector.tensor_scalar(
+                    out=running_top[group][:], in0=sim_first[step][:], scalar1=bar, scalar2=None,
+                    op0=ALU.add,
+                )
+            else:
+                nc.vector.scalar_tensor_tensor(
+                    out=running_top[group][:], in0=sim_first[step][:], scalar=bar,
+                    in1=running_top[group][:], op0=ALU.add, op1=ALU.max,
+                )
+
+        def finish_top(step):
+            if in_first_sweep(step) and step % TOKENS == TOKENS - 1:
+                group = step // TOKENS
                 nc.vector.tensor_reduce(
-                    out=top_f,
-                    in_=sim_first[step][:].rearrange("a (v b) -> a b v", v=FRAMES),
+                    out=top[:, group_videos(group)],
+                    in_=running_top[group][:].rearrange("a (v b) -> a b v", v=FRAMES),
                     axis=INNERMOST,
                     op=ALU.max,
                 )
-            if in_second_sweep(step):
-                if step % PAIR == 0:
-                    pair_shape = [P, PAIR, GROUP_COLS]
-                    token_tiles[step // PAIR] = (
-                        pair_work.tile(pair_shape, F32, tag="dev_t", name="dev_t"),
-                        pair_work.tile(pair_shape, F32, tag="wgt_t", name="wgt_t"),
-                    )
-                nc.vector.scalar_tensor_tensor(
-                    out=token_tiles[step // PAIR][0][:, step % PAIR, :],
-                    in0=sim_second[step][:],
-                    scalar=mask[:, token : token + 1],
-                    in1=token_top[:, group - 1, :],
-                    op0=ALU.mult,
-                    op1=ALU.subtract,
-                )
-            if in_first_sweep(step):
-                sim = sim_first[step]
-                if step % QUAD == 0:
-                    quad_shape = [P, FRAMES, QUAD, GROUP_VIDEOS]
-                    frame_tiles[step // QUAD] = (
-                        quad_work.tile(quad_shape, F32, tag="dev_f", name="dev_f"),
-                        quad_work.tile(quad_shape, F32, tag="wgt_f", name="wgt_f"),
-                    )
-                nc.vector.tensor_tensor(
-                    out=frame_tiles[step // QUAD][0][:, :, step % QUAD, :],
-                    in0=sim[:].rearrange("a (v b) -> a v b", v=FRAMES),
-                    in1=top_f.unsqueeze(1).to_broadcast([P, FRAMES, GROUP_VIDEOS]),
-                    op=ALU.subtract,
-                )
-                bar = barred[:, token : token + 1]
-                top_t = token_top[:, group, :]
-                if token == 0:
-                    nc.vector.tensor_scalar(
-                        out=top_t, in0=sim[:], scalar1=bar, scalar2=None, op0=ALU.add
-                    )
-                else:
-                    nc.vector.scalar_tensor_tensor(
-                        out=top_t, in0=sim[:], scalar=bar, in1=top_t, op0=ALU.add, op1=ALU.max
-                    )
-                if token == TOKENS - 1:
-                    nc.vector.tensor_scalar_mul(out=top_t, in0=top_t, scalar1=mask_top[:, 0:1])
 
         def weigh(step):
-            token = step % TOKENS
-            if in_second_sweep(step):
-                dev_t, wgt_t = token_tiles[step // PAIR]
-                nc.scalar.activation(
-                    out=wgt_t[:, step % PAIR, :],
-                    in_=dev_t[:, step % PAIR, :],
-                    func=FN.Exp,
-                    scale=TAU,
-                    bias=barred[:, token : token + 1],
-                )
-            if in_first_sweep(step):
-                dev_f, wgt_f = frame_tiles[step // QUAD]
-                nc.scalar.activation(
-                    out=wgt_f[:, :, step % QUAD, :],
-                    in_=dev_f[:, :, step % QUAD, :],
-                    func=FN.Exp,
-                    scale=sharp_mask[:, token : token + 1],
-                )
-
-        def form_products(step):
-            if step % PAIR != PAIR - 1:
+            if not in_second_sweep(step):
                 return
-            if in_second_sweep(step):
-                dev_t, wgt_t = token_tiles[step // PAIR]
-                nc.gpsimd.tensor_tensor(out=dev_t[:], in0=dev_t[:], in1=wgt_t[:], op=ALU.mult)
-            if in_first_sweep(step):
-                dev_f, wgt_f = frame_tiles[step // QUAD]
-                slots = slice(step % QUAD - (PAIR - 1), step % QUAD + 1)
-                nc.gpsimd.tensor_tensor(
-                    out=dev_f[:, :, slots, :],
-                    in0=dev_f[:, :, slots, :],
-                    in1=wgt_f[:, :, slots, :],
-                    op=ALU.mult,
+            token = step % TOKENS
+            if step % QUAD == 0:
+                quad_shape = [P, FRAMES, QUAD, GROUP_VIDEOS]
+                quad_tiles[step // QUAD] = (
+                    quad_work.tile(quad_shape, F32, tag="quad_weights", name="quad_weights"),
+                    quad_work.tile(quad_shape, F32, tag="quad_products", name="quad_products"),
+                )
+            weights[step] = token_work.tile([P, GROUP_COLS], F32, tag="weight", name="weight")
+            by_frame = "a (v b) -> a v b"
+            for target, source in (
+                (weights[step][:], deviations[step][:]),
+                (
+                    quad_tiles[step // QUAD][0][:, :, step % QUAD, :],
+                    deviations[step][:].rearrange(by_frame, v=FRAMES),
+                ),
+            ):
+                nc.scalar.activation(
+                    out=target, in_=source, func=FN.Exp,
+                    scale=sharp_mask[:, token : token + 1], bias=barred[:, token : token + 1],
                 )
 
-        def add_up_tokens(step):
+        def form_product(step):
+            if not in_second_sweep(step):
+                return
+            nc.vector.tensor_tensor(
+                out=quad_tiles[step // QUAD][1][:, :, step % QUAD, :],
+                in0=sim_second[step][:].rearrange("a (v b) -> a v b", v=FRAMES),
+                in1=weights[step][:].rearrange("a (v b) -> a v b", v=FRAMES),
+                op=ALU.mult,
+            )
+
+        def add_up_products(step):
+            if not in_second_sweep(step):
+                return
+            group = step // TOKENS - 1
+            products = quad_tiles[step // QUAD][1]
+            if step % TOKENS == 0:
+                product_sums[group] = group_work.tile(
+                    [P, FRAMES, GROUP_VIDEOS], F32, tag="product_sums", name="product_sums"
+                )
+                return
+            acc = product_sums[group]
+            so_far = products[:, :, 0, :] if step % TOKENS == 1 else acc[:]
+            nc.gpsimd.tensor_tensor(
+                out=acc[:], in0=so_far, in1=products[:, :, step % QUAD, :], op=ALU.add
+            )
+
+        def add_up_weights(step):
             if not in_second_sweep(step):
                 return
             token = step % TOKENS
             group = step // TOKENS - 1
             if token == 0:
-                group_banks[group] = (
-                    psum.tile([P, GROUP_COLS], F32, tag="weight_sums", name="weight_sums", bufs=1),
-                    psum.tile([P, GROUP_COLS], F32, tag="product_sums", name="product_sums", bufs=1),
+                weight_banks[group] = psum.tile(
+                    [P, BLOCKS, P], F32, tag="weight_sums", name="weight_sums", bufs=1
                 )
-            dev_t, wgt_t = token_tiles[step // PAIR]
-            for plane, terms in enumerate((wgt_t, dev_t)):
-                acc = group_banks[group][plane]
-                for k in range(BLOCKS):
-                    cols = slice(k * P, (k + 1) * P)
-                    transpose_add(
-                        acc[:, cols],
-                        terms[:, step % PAIR, cols],
-                        token == 0 and k == 0,
-                        token == TOKENS - 1 and k == BLOCKS - 1,
-                    )
-                if token == TOKENS - 1:
-                    first_col = token_sum_col(group)
-                    nc.scalar.copy(out=sums[:, plane, first_col : first_col + GROUP_COLS], in_=acc[:])
+            for k in range(BLOCKS):
+                transpose_add(
+                    weight_banks[group][:, k, :],
+                    weights[step][:, k * P : (k + 1) * P],
+                    token == 0 and k == 0,
+                    token == TOKENS - 1 and k == BLOCKS - 1,
+                )
+            if token == TOKENS - 1:
+                token_sums[group] = finish.tile([P, 2, BLOCKS, P], F32, tag="sums", name="token_sums")
+                store(token_sums[group], 0, slice(0, BLOCKS), weight_banks[group][:])
+
+        def store(sums, plane, blocks, source):
+            nc.scalar.activation(
+                out=sums[:, plane, blocks, :], in_=source, func=FN.Identity,
+                bias=nudge[:, plane : plane + 1],
+            )
 
         def add_up_frames(step):
-            if not in_first_sweep(step):
+            if not in_second_sweep(step):
                 return
             quad = step // QUAD
             plane = (step % QUAD) // 2
             first_frame = (step % 2) * (FRAMES // 2)
             if step % QUAD == 0:
-                quad_banks[quad] = psum.tile([P, 2, P], F32, tag="quad_sums", name="quad_sums")
-            terms = frame_tiles[quad][1 - plane]
+                quad_banks[quad] = psum.tile([P, 2, 1, P], F32, tag="quad_sums", name="quad_sums", bufs=1)
             for v in range(first_frame, first_frame + FRAMES // 2):
                 transpose_add(
-                    quad_banks[quad][:, plane, :],
-                    terms[:, v, :, :].rearrange("a s b -> a (s b)"),
+                    quad_banks[quad][:, plane, 0, :],
+                    quad_tiles[quad][plane][:, v, :, :].rearrange("a s b -> a (s b)"),
                     v == 0,
                     v == FRAMES - 1,
                 )
 
         def store_frame_sums(step):
-            if in_first_sweep(step) and step % QUAD == QUAD - 1:
-                first_col = frame_sum_col(step // TOKENS) + (step % TOKENS) // QUAD * P
-                nc.scalar.copy(
-                    out=sums[:, :, first_col : first_col + P], in_=quad_banks[step // QUAD][:]
+            if not in_second_sweep(step) or step % QUAD != QUAD - 1:
+                return
+            group = step // TOKENS - 1
+            half = step % TOKENS // HALF
+            block = step % HALF // QUAD
+            if block == 0:
+                frame_sums[group, half] = finish.tile(
+                    [P, 2, BLOCKS, P], F32, tag="sums", name="frame_sums"
+                )
+            for plane in range(2):
+                store(
+                    frame_sums[group, half], plane, slice(block, block + 1),
+                    quad_banks[step // QUAD][:, plane, :, :],
                 )
 
         def pipeline_step(step):
             multiply(step + 1)
-            subtract_tops(step)
+            store_frame_sums(step - FRAME_LAG - 1)
+            subtract_top(step)
+            raise_top(step)
             weigh(step)
-            form_products(step - 1)
-            add_up_tokens(step - SUM_LAG)
-            add_up_frames(step - SUM_LAG)
-            store_frame_sums(step - SUM_LAG - 1)
+            form_product(step - 1)
+            finish_top(step)
+            add_up_products(step - 1)
+            add_up_weights(step - TOKEN_LAG)
+            add_up_frames(step - FRAME_LAG)
 
         with tc.tile_pool(name="text_prep", bufs=2) as text_prep:
             text_raw = text_prep.tile([P, TOKENS, FEATURES], BF16, name="text_raw", bufs=1)
@@ -374,179 +396,140 @@ def tile_mug_head_kernel(tc, text_feat, video_feat, text_mask, out):
                     prepare_text_quad((step + 1) // QUAD + 1)
                 pipeline_step(step)
 
-        with tc.manual_schedule():
-            for step in range(TOKENS - 1, FIRST_STEPS - 1):
-                pipeline_step(step)
+        finish = pools.enter_context(tc.tile_pool(name="finish", bufs=4))
 
-        finish = pools.enter_context(tc.tile_pool(name="finish", bufs=2))
+        def turn_top_pieces(group):
+            made = {}
 
-        def turn_back(made, first_col):
-            made["bank"] = psum.tile([P, BLOCKS * P], F32, tag="first", name="turned_back")
-            for k in range(BLOCKS):
-                block = sums[:, 1, first_col + k * P : first_col + (k + 1) * P]
-                nc.tensor.transpose(made["bank"][:, k * P : (k + 1) * P], block, ident_f32[:])
+            def repeat():
+                made["repeated"] = finish.tile([P, QUAD, GROUP_VIDEOS], F32, tag="repeated", name="repeated", bufs=2)
+                nc.scalar.copy(
+                    out=made["repeated"][:],
+                    in_=top[:, group_videos(group)].unsqueeze(1).to_broadcast([P, QUAD, GROUP_VIDEOS]),
+                )
 
-        def division_pieces(first_col, last_col):
-            weights = sums[:, 0, first_col:last_col]
+            def turn():
+                made["bank"] = psum.tile([P, P], F32, tag="turned", name="turned_top", bufs=1)
+                nc.tensor.transpose(
+                    made["bank"][:], made["repeated"][:].rearrange("a s b -> a (s b)"), ident_f32[:]
+                )
+
+            def keep_turned():
+                nc.scalar.copy(out=top_turned[:, group, :], in_=made["bank"][:])
+
+            return [repeat, turn, keep_turned]
+
+        def product_sum_pieces(group):
+            made = {}
+
+            def turn():
+                made["bank"] = psum.tile([P, BLOCKS, P], F32, tag="turned", name="turned_products", bufs=1)
+                columns = product_sums[group][:].rearrange("a v b -> a (v b)")
+                for k in range(BLOCKS):
+                    nc.tensor.transpose(
+                        made["bank"][:, k, :], columns[:, k * P : (k + 1) * P], ident_f32[:]
+                    )
+
+            def keep_turned():
+                store(token_sums[group], 1, slice(0, BLOCKS), made["bank"][:])
+
+            return [turn, keep_turned]
+
+        def pooling_pieces(sums, group, entry):
+            made = {}
 
             def invert():
-                nc.scalar.activation(out=weights, in_=weights, func=FN.Ln)
-                nc.scalar.activation(out=weights, in_=weights, func=FN.Exp, scale=-1.0)
+                made["weights"] = sums()[:, 0, :, :]
+                made["means"] = sums()[:, 1, :, :]
+                nc.scalar.activation(out=made["weights"], in_=made["weights"], func=FN.Ln)
 
-            def multiply_by_inverse(col):
-                cols = slice(col, col + GROUP_COLS)
+            def invert_more():
+                nc.scalar.activation(out=made["weights"], in_=made["weights"], func=FN.Exp, scale=-1.0)
+
+            def divide():
                 nc.gpsimd.tensor_tensor(
-                    out=sums[:, 1, cols], in0=sums[:, 1, cols], in1=sums[:, 0, cols], op=ALU.mult
+                    out=made["means"], in0=made["means"], in1=made["weights"], op=ALU.mult
                 )
 
-            pieces = [invert]
-            for col in range(first_col, last_col, GROUP_COLS):
-                pieces.append(lambda col=col: multiply_by_inverse(col))
-            return pieces
-
-        def new_statistics(name):
-            return {
-                "top": finish.tile([P, P], F32, name=name + "_top", bufs=1),
-                "weights": finish.tile([P, P], F32, name=name + "_weights", bufs=1),
-                "products": finish.tile([P, P], F32, name=name + "_products", bufs=1),
-            }
-
-        def pooling_pieces(made, count, group, statistics):
-            shape = [P, GROUP_VIDEOS, count]
-            videos = slice(group * GROUP_VIDEOS, (group + 1) * GROUP_VIDEOS)
-            top = statistics["top"][:, videos]
-
-            def find_top():
-                nc.vector.tensor_reduce(out=top, in_=made["values"][:], axis=INNERMOST, op=ALU.max)
-
-            def weigh_deviations():
-                made["dev"] = finish.tile(shape, F32, tag="dev%d" % count, name="dev")
-                made["wgt"] = finish.tile(shape, F32, tag="wgt%d" % count, name="wgt")
+            def deviate():
                 nc.vector.tensor_tensor(
-                    out=made["dev"][:],
-                    in0=made["values"][:],
-                    in1=top.unsqueeze(2).to_broadcast(shape),
+                    out=made["means"], in0=made["means"],
+                    in1=top_turned[:, group, :].unsqueeze(1).to_broadcast([P, BLOCKS, P]),
                     op=ALU.subtract,
                 )
-                nc.scalar.activation(out=made["wgt"][:], in_=made["dev"][:], func=FN.Exp, scale=TAU)
 
-            def form_product():
+            def weigh_means():
+                nc.scalar.activation(
+                    out=made["weights"], in_=made["means"], func=FN.Exp, scale=sharp_top[:, 0:1]
+                )
+
+            def form_products():
                 nc.gpsimd.tensor_tensor(
-                    out=made["dev"][:], in0=made["dev"][:], in1=made["wgt"][:], op=ALU.mult
+                    out=made["means"], in0=made["means"], in1=made["weights"], op=ALU.mult
                 )
 
-            def add_weights():
+            def turn_back():
+                bank = psum.tile([P, 2, QUAD, GROUP_VIDEOS], F32, tag="turned", name="turned_back", bufs=1)
+                for plane in range(2):
+                    for k in range(BLOCKS):
+                        transpose_add(
+                            bank[:, plane, :, :].rearrange("a s b -> a (s b)"),
+                            sums()[:, plane, k, :],
+                            k == 0,
+                            k == BLOCKS - 1,
+                        )
                 nc.vector.tensor_reduce(
-                    out=statistics["weights"][:, videos], in_=made["wgt"][:],
-                    axis=INNERMOST, op=ALU.add,
-                )
-
-            def add_products():
-                nc.vector.tensor_reduce(
-                    out=statistics["products"][:, videos], in_=made["dev"][:],
-                    axis=INNERMOST, op=ALU.add,
-                )
-
-            return [find_top, weigh_deviations, form_product, add_weights, add_products]
-
-        def pooled_mean(statistics):
-            nc.vector.reciprocal(out=statistics["weights"][:], in_=statistics["weights"][:])
-            nc.vector.tensor_tensor(
-                out=statistics["products"][:], in0=statistics["products"][:],
-                in1=statistics["weights"][:], op=ALU.mult,
-            )
-            nc.vector.tensor_tensor(
-                out=statistics["products"][:], in0=statistics["products"][:],
-                in1=statistics["top"][:], op=ALU.add,
-            )
-            return statistics["products"]
-
-        def text_to_video_pieces(group, statistics):
-            made = {}
-            tokens_of_bank = BLOCKS * QUAD
-
-            def add_frame_top(first):
-                if first == 0:
-                    made["raw"] = finish.tile(
-                        [P, TOKENS, GROUP_VIDEOS], F32, tag="t2v_raw", name="t2v_raw"
-                    )
-                tokens = slice(first, first + tokens_of_bank)
-                nc.vector.tensor_tensor(
-                    out=made["raw"][:, tokens, :],
-                    in0=made["bank"][:].rearrange("a (t b) -> a t b", b=GROUP_VIDEOS),
-                    in1=frame_top[:, group, tokens, :],
+                    out=statistics[:, entry, :, group_videos(group)],
+                    in_=bank[:].rearrange("a q s b -> a q b s"),
+                    axis=INNERMOST,
                     op=ALU.add,
                 )
 
-            def mask_and_bar():
-                made["values"] = finish.tile([P, GROUP_VIDEOS, TOKENS], F32, tag="t2v", name="t2v")
-                for token in range(TOKENS):
-                    nc.scalar.activation(
-                        out=made["values"][:, :, token],
-                        in_=made["raw"][:, token, :],
-                        func=FN.Identity,
-                        scale=mask[:, token : token + 1],
-                        bias=barred[:, token : token + 1],
-                    )
+            return [invert, invert_more, divide, deviate, weigh_means, form_products, turn_back]
 
-            pieces = []
-            for first in range(0, TOKENS, tokens_of_bank):
-                first_col = frame_sum_col(group) + first // QUAD * P
-                pieces.append(lambda first_col=first_col: turn_back(made, first_col))
-                pieces.append(lambda first=first: add_frame_top(first))
-            pieces.append(mask_and_bar)
-            pieces.extend(pooling_pieces(made, TOKENS, group, statistics))
-            return pieces
-
-        def video_to_text_pieces(group, statistics):
-            made = {}
-
-            def add_token_top():
-                made["values"] = finish.tile([P, GROUP_VIDEOS, FRAMES], F32, tag="v2t", name="v2t")
-                nc.vector.tensor_tensor(
-                    out=made["values"][:],
-                    in0=made["bank"][:].rearrange("a (v b) -> a b v", v=FRAMES),
-                    in1=token_top[:, group, :].rearrange("a (v b) -> a b v", v=FRAMES),
-                    op=ALU.add,
-                )
-
-            pieces = [lambda: turn_back(made, token_sum_col(group)), add_token_top]
-            pieces.extend(pooling_pieces(made, FRAMES, group, statistics))
-            return pieces
-
-        over_tokens = new_statistics("over_tokens")
-        over_frames = new_statistics("over_frames")
-        last_phase_col = token_sum_col(GROUPS - 2)
         waiting = []
-        for piece in division_pieces(0, last_phase_col):
-            waiting.append((FIRST_STEPS - 1, piece))
-        for phase in range(GROUPS + 1):
-            ready = max(FIRST_STEPS - 1, (phase + 1) * TOKENS + SUM_LAG)
-            pieces = []
-            if phase == GROUPS - 1:
-                pieces.extend(division_pieces(last_phase_col, token_sum_col(GROUPS - 1)))
-            if phase == GROUPS:
-                pieces.extend(division_pieces(token_sum_col(GROUPS - 1), SUM_COLS))
-            if phase < GROUPS:
-                pieces.extend(text_to_video_pieces(phase, over_tokens))
-            if phase > 0:
-                pieces.extend(video_to_text_pieces(phase - 1, over_frames))
-            for piece in pieces:
-                waiting.append((ready, piece))
+        for group in range(GROUPS):
+            first_step = (group + 1) * TOKENS
+            for piece in turn_top_pieces(group):
+                waiting.append((first_step, piece))
+            half_done = first_step + HALF + FRAME_LAG
+            for piece in pooling_pieces(lambda group=group: frame_sums[group, 0], group, 0):
+                waiting.append((half_done, piece))
+            all_done = first_step + TOKENS + FRAME_LAG
+            for piece in product_sum_pieces(group):
+                waiting.append((all_done, piece))
+            by_tokens = pooling_pieces(lambda group=group: frame_sums[group, 1], group, 1)
+            by_frames = pooling_pieces(lambda group=group: token_sums[group], group, 2)
+            for pair in zip(by_tokens, by_frames):
+                for piece in pair:
+                    waiting.append((all_done, piece))
 
-        served = 0
-        for step in range(FIRST_STEPS - 1, STEPS + SUM_LAG + 1):
-            pipeline_step(step)
-            for turn in range(PIECES_PER_STEP):
-                if served < len(waiting) and waiting[served][0] <= step:
-                    waiting[served][1]()
-                    served += 1
-        for ready, piece in waiting[served:]:
-            piece()
+        with tc.manual_schedule():
+            served = 0
+            for step in range(TOKENS - 1, STEPS + FRAME_LAG + 1):
+                pipeline_step(step)
+                for turn in range(PIECES_PER_STEP):
+                    if served < len(waiting) and waiting[served][0] <= step:
+                        waiting[served][1]()
+                        served += 1
+            for ready, piece in waiting[served:]:
+                piece()
 
-        result = finish.tile([P, P], F32, name="result", bufs=1)
-        nc.vector.tensor_tensor(
-            out=result[:], in0=pooled_mean(over_tokens)[:], in1=pooled_mean(over_frames)[:], op=ALU.add
-        )
-        nc.vector.tensor_scalar_mul(out=result[:], in0=result[:], scalar1=0.5)
-        nc.sync.dma_start(out=out, in_=result[:])
+            over_tokens = statistics[:, 0, :, :]
+            nc.vector.tensor_tensor(
+                out=over_tokens, in0=over_tokens, in1=statistics[:, 1, :, :], op=ALU.add
+            )
+            result = finish.tile([P, 2, P], F32, name="result", bufs=1)
+            for part, entry in enumerate((0, 2)):
+                nc.vector.reciprocal(out=result[:, part, :], in_=statistics[:, entry, 0, :])
+                nc.vector.tensor_tensor(
+                    out=result[:, part, :], in0=result[:, part, :], in1=statistics[:, entry, 1, :],
+                    op=ALU.mult,
+                )
+            total = result[:, 0, :]
+            nc.vector.tensor_tensor(out=total, in0=total, in1=result[:, 1, :], op=ALU.add)
+            nc.vector.scalar_tensor_tensor(
+                out=total, in0=total, scalar=0.5, in1=top[:], op0=ALU.mult, op1=ALU.add
+            )
+            nc.vector.tensor_scalar_mul(out=total, in0=total, scalar1=mask_top[:, 0:1])
+            nc.sync.dma_start(out=out, in_=total)

@@ -28,13 +28,15 @@ GROUP_VIDEOS = P // GROUPS
 GROUP_COLS = FRAMES * GROUP_VIDEOS
 BLOCKS = GROUP_COLS // P
 QUAD = 4
-HALF = QUAD * BLOCKS
+QUADS = TOKENS // QUAD
+UNITS = QUADS // BLOCKS + 1
+TOKEN_UNIT = UNITS - 1
 
 FIRST_STEPS = GROUPS * TOKENS
 STEPS = FIRST_STEPS + TOKENS
 FRAME_LAG = 4
 TOKEN_LAG = 2
-PIECES_PER_STEP = 2
+PIECES_PER_STEP = 3
 
 FLOPS = 2 * (P * TOKENS) * (P * FRAMES) * FEATURES
 
@@ -48,8 +50,6 @@ def tile_mug_head_kernel(tc, text_feat, video_feat, text_mask, out):
 
         ident_f32 = consts.tile([P, P], F32, name="ident_f32")
         make_identity(nc, ident_f32[:])
-        ident_bf16 = consts.tile([P, P], BF16, name="ident_bf16")
-        make_identity(nc, ident_bf16[:])
 
         mask_bf16 = consts.tile([P, TOKENS], BF16, name="mask_bf16")
         nc.sync.dma_start(out=mask_bf16[:], in_=text_mask)
@@ -78,79 +78,14 @@ def tile_mug_head_kernel(tc, text_feat, video_feat, text_mask, out):
         video_scales = keep.tile([P, GROUPS * GROUP_COLS], U8, name="video_scales", align_bytes=64)
         top = keep.tile([P, P], F32, name="top")
         top_turned = keep.tile([P, GROUPS, P], F32, name="top_turned")
-        statistics = keep.tile([P, 3, 2, P], F32, name="statistics")
+        sums = keep.tile([P, GROUPS, 2, UNITS * BLOCKS, P], F32, name="sums")
+        statistics = keep.tile([P, UNITS, 2, P], F32, name="statistics")
 
         def transpose_add(acc, block, start, stop):
             nc.tensor.matmul(
                 out=acc, lhsT=block, rhs=ident_f32[:], is_transpose=True, start=start, stop=stop
             )
 
-        def inverse_norms(pool, raw, count):
-            by_scalar = pool.tile([P, count // 2], F32, name="squares_by_scalar", bufs=1)
-            by_vector = pool.tile([P, count // 2], F32, name="squares_by_vector", bufs=1)
-            for i in range(count):
-                total = slice(i // 2, i // 2 + 1)
-                if i % 2 == 0:
-                    squares = pool.tile([P, FEATURES], BF16, tag="squares_s", name="squares_s")
-                    nc.scalar.activation(
-                        out=squares[:], in_=raw[:, i, :], func=FN.Square, accum_out=by_scalar[:, total]
-                    )
-                else:
-                    squares = pool.tile([P, FEATURES], F32, tag="squares_v", name="squares_v")
-                    nc.vector.scalar_tensor_tensor(
-                        out=squares[:], in0=raw[:, i, :], scalar=1.0, in1=raw[:, i, :],
-                        op0=ALU.mult, op1=ALU.mult, accum_out=by_vector[:, total],
-                    )
-            inverse = pool.tile([P, 2, count // 2], F32, name="inverse", bufs=1)
-            for parity, square_sum in enumerate((by_scalar, by_vector)):
-                nc.vector.tensor_scalar_max(out=square_sum[:], in0=square_sum[:], scalar1=EPS * EPS)
-                nc.scalar.sqrt(out=inverse[:, parity, :], in_=square_sum[:])
-                nc.vector.reciprocal(out=inverse[:, parity, :], in_=inverse[:, parity, :])
-            return inverse
-
-        def features_to_partitions(rows):
-            bank = psum.tile([P, PACK, P], BF16, tag="second", name="turned_rows", bufs=3)
-            for j in range(PACK):
-                nc.tensor.transpose(bank[:, j, :], rows[:, j * P : (j + 1) * P], ident_bf16[:])
-            return bank
-
-        with tc.tile_pool(name="video_prep", bufs=2) as video_prep:
-            video_raw = video_prep.tile([P, FRAMES, FEATURES], BF16, name="video_raw", bufs=1)
-            for first in range(0, FRAMES, 4):
-                nc.sync.dma_start(
-                    out=video_raw[:, first : first + 4, :], in_=video_feat[:, first : first + 4, :]
-                )
-            warm = video_prep.tile([P, 1], F32, name="warm", bufs=1)
-            nc.vector.memset(warm[:], 1.0)
-            nc.scalar.sqrt(out=warm[:], in_=warm[:])
-            video_inverse = inverse_norms(video_prep, video_raw, FRAMES)
-            video_grouped = video_prep.tile(
-                [P, GROUPS, FRAMES, GROUP_VIDEOS, PACK], BF16,
-                name="video_grouped", bufs=1, align_bytes=64,
-            )
-            for v in range(FRAMES):
-                rows = video_prep.tile([P, FEATURES], BF16, tag="rows", name="rows", bufs=3)
-                nc.vector.tensor_scalar_mul(
-                    out=rows[:].rearrange("b (j p) -> b j p", j=PACK),
-                    in0=video_raw[:, v, :].rearrange("b (p j) -> b j p", j=PACK),
-                    scalar1=video_inverse[:, v % 2, v // 2 : v // 2 + 1],
-                )
-                bank = features_to_partitions(rows)
-                copy = nc.scalar.copy if v % 2 == 0 else nc.vector.tensor_copy
-                copy(
-                    out=video_grouped[:, :, v, :, :],
-                    in_=bank[:].rearrange("p j (g b) -> p g b j", g=GROUPS),
-                )
-            for group in range(GROUPS):
-                cols = slice(group * GROUP_COLS, (group + 1) * GROUP_COLS)
-                nc.vector.quantize_mx(
-                    out=video_codes[:, cols].bitcast(FP8X4),
-                    scales=video_scales[:, cols],
-                    in_=video_grouped[:, group, :, :, :].rearrange("p v b j -> p (v b j)"),
-                )
-
-        quad_work = pools.enter_context(tc.tile_pool(name="quad_work", bufs=3))
-        token_work = pools.enter_context(tc.tile_pool(name="token_work", bufs=4))
         group_work = pools.enter_context(tc.tile_pool(name="group_work", bufs=2))
 
         def similarities(token, group, tag, bufs, times):
@@ -178,8 +113,6 @@ def tile_mug_head_kernel(tc, text_feat, video_feat, text_mask, out):
         product_sums = {}
         quad_banks = {}
         weight_banks = {}
-        frame_sums = {}
-        token_sums = {}
 
         def in_first_sweep(step):
             return 0 <= step < FIRST_STEPS
@@ -305,12 +238,14 @@ def tile_mug_head_kernel(tc, text_feat, video_feat, text_mask, out):
                     token == TOKENS - 1 and k == BLOCKS - 1,
                 )
             if token == TOKENS - 1:
-                token_sums[group] = finish.tile([P, 2, BLOCKS, P], F32, tag="sums", name="token_sums")
-                store(token_sums[group], 0, slice(0, BLOCKS), weight_banks[group][:])
+                store(group, 0, unit_blocks(TOKEN_UNIT), weight_banks[group][:])
 
-        def store(sums, plane, blocks, source):
+        def unit_blocks(unit):
+            return slice(unit * BLOCKS, (unit + 1) * BLOCKS)
+
+        def store(group, plane, blocks, source):
             nc.scalar.activation(
-                out=sums[:, plane, blocks, :], in_=source, func=FN.Identity,
+                out=sums[:, group, plane, blocks, :], in_=source, func=FN.Identity,
                 bias=nudge[:, plane : plane + 1],
             )
 
@@ -333,16 +268,10 @@ def tile_mug_head_kernel(tc, text_feat, video_feat, text_mask, out):
         def store_frame_sums(step):
             if not in_second_sweep(step) or step % QUAD != QUAD - 1:
                 return
-            group = step // TOKENS - 1
-            half = step % TOKENS // HALF
-            block = step % HALF // QUAD
-            if block == 0:
-                frame_sums[group, half] = finish.tile(
-                    [P, 2, BLOCKS, P], F32, tag="sums", name="frame_sums"
-                )
+            block = step % TOKENS // QUAD
             for plane in range(2):
                 store(
-                    frame_sums[group, half], plane, slice(block, block + 1),
+                    step // TOKENS - 1, plane, slice(block, block + 1),
                     quad_banks[step // QUAD][:, plane, :, :],
                 )
 
@@ -358,115 +287,201 @@ def tile_mug_head_kernel(tc, text_feat, video_feat, text_mask, out):
             add_up_weights(step - TOKEN_LAG)
             add_up_frames(step - FRAME_LAG)
 
-        with tc.tile_pool(name="text_prep", bufs=2) as text_prep:
-            text_raw = text_prep.tile([P, TOKENS, FEATURES], BF16, name="text_raw", bufs=1)
-            for first in range(0, TOKENS, 8):
-                nc.sync.dma_start(
-                    out=text_raw[:, first : first + 8, :], in_=text_feat[:, first : first + 8, :]
-                )
-            text_inverse = inverse_norms(text_prep, text_raw, TOKENS)
+        first_text = FRAMES // QUAD
+        batches = first_text + QUADS
+        rows_of = {}
+        squares_of = {}
+        normal_of = {}
+        grouped_of = {}
 
-            def prepare_text_quad(quad):
-                grouped = text_prep.tile(
-                    [P, QUAD, P, PACK], BF16, tag="text_grouped", name="text_grouped", align_bytes=64
-                )
-                for slot in range(QUAD):
-                    token = quad * QUAD + slot
-                    rows = text_prep.tile([P, FEATURES], BF16, tag="rows", name="rows", bufs=3)
-                    nc.scalar.activation(
-                        out=rows[:].rearrange("a (j p) -> a j p", j=PACK),
-                        in_=text_raw[:, token, :].rearrange("a (p j) -> a j p", j=PACK),
-                        func=FN.Copy,
-                        scale=text_inverse[:, token % 2, token // 2 : token // 2 + 1],
+        with tc.manual_schedule(), tc.tile_pool(name="prep", bufs=3) as prep:
+            warm = prep.tile([P, 1], F32, name="warm", bufs=1)
+            nc.vector.memset(warm[:], 1.0)
+            nc.scalar.sqrt(out=warm[:], in_=warm[:])
+            video_grouped = prep.tile(
+                [P, GROUPS * GROUP_COLS * PACK], BF16, name="video_grouped", bufs=1, align_bytes=64
+            )
+
+            def load(batch):
+                rows_of[batch] = prep.tile([P, QUAD, FEATURES], BF16, tag="raw", name="raw", bufs=batches)
+                if batch < first_text:
+                    source = video_feat[:, batch * QUAD : (batch + 1) * QUAD, :]
+                else:
+                    first = (batch - first_text) * QUAD
+                    source = text_feat[:, first : first + QUAD, :]
+                nc.sync.dma_start(out=rows_of[batch][:], in_=source)
+
+            def add_up_squares(batch):
+                sums_of_squares = prep.tile([P, QUAD], F32, tag="squares", name="sums_of_squares")
+                squares_of[batch] = sums_of_squares
+                for i in range(QUAD):
+                    row = rows_of[batch][:, i, :]
+                    total = sums_of_squares[:, i : i + 1]
+                    if i % 2 == 0 or batch >= first_text + BLOCKS - 1:
+                        scratch = prep.tile([P, FEATURES], BF16, tag="scratch_s", name="scratch_s")
+                        nc.scalar.activation(out=scratch[:], in_=row, func=FN.Square, accum_out=total)
+                    else:
+                        scratch = prep.tile([P, FEATURES], BF16, tag="scratch_v", name="scratch_v")
+                        nc.vector.scalar_tensor_tensor(
+                            out=scratch[:], in0=row, scalar=1.0, in1=row,
+                            op0=ALU.mult, op1=ALU.mult, accum_out=total,
+                        )
+
+            def invert_norms(batch):
+                norms = squares_of[batch]
+                nc.scalar.sqrt(out=norms[:], in_=norms[:])
+                nc.vector.tensor_scalar_max(out=norms[:], in0=norms[:], scalar1=EPS)
+                nc.vector.reciprocal(out=norms[:], in_=norms[:])
+
+            def normalise(batch):
+                normal = prep.tile([P, QUAD, FEATURES], BF16, tag="normal", name="normal")
+                normal_of[batch] = normal
+                for i in range(QUAD):
+                    inverse = squares_of[batch][:, i : i + 1]
+                    if batch < first_text:
+                        nc.vector.tensor_scalar_mul(
+                            out=normal[:, i, :], in0=rows_of[batch][:, i, :], scalar1=inverse
+                        )
+                    else:
+                        nc.gpsimd.tensor_scalar(
+                            out=normal[:, i, :], in0=rows_of[batch][:, i, :],
+                            scalar1=inverse, scalar2=0.0, op0=ALU.mult, op1=ALU.add,
+                        )
+
+            def turn(batch):
+                if batch >= first_text:
+                    grouped_of[batch] = prep.tile(
+                        [P, QUAD * P * PACK], BF16, tag="text_grouped", name="text_grouped", align_bytes=64
                     )
-                    bank = features_to_partitions(rows)
-                    nc.scalar.copy(
-                        out=grouped[:, slot, :, :], in_=bank[:].rearrange("p j a -> p a j")
-                    )
-                cols = slice(quad * QUAD * P, (quad + 1) * QUAD * P)
+                for pair in range(0, QUAD, 2):
+                    bank = psum.tile([P, 2, 2, P], F32, tag="second", name="turned_rows", bufs=3)
+                    for i in range(2):
+                        words = normal_of[batch][:, pair + i, :].bitcast(F32)
+                        for u in range(2):
+                            nc.tensor.transpose(
+                                bank[:, i, u, :], words[:, u : FEATURES // 2 : 2], ident_f32[:]
+                            )
+                    if batch >= first_text:
+                        target = grouped_of[batch][:].bitcast(F32)
+                        nc.scalar.copy(
+                            out=target.rearrange("p (s a u) -> p s a u", s=QUAD, u=2)[:, pair : pair + 2],
+                            in_=bank[:].rearrange("p s u a -> p s a u"),
+                        )
+                    else:
+                        target = video_grouped[:].bitcast(F32)
+                        target = target.rearrange("p (g v b u) -> p g v b u", g=GROUPS, v=FRAMES, u=2)
+                        for i in range(2):
+                            nc.scalar.copy(
+                                out=target[:, :, batch * QUAD + pair + i],
+                                in_=bank[:, i, :, :].rearrange("p u (g b) -> p g b u", g=GROUPS),
+                            )
+
+            def quantise_videos(group):
+                cols = slice(group * GROUP_COLS, (group + 1) * GROUP_COLS)
+                values = slice(group * GROUP_COLS * PACK, (group + 1) * GROUP_COLS * PACK)
                 nc.vector.quantize_mx(
-                    out=text_codes[:, cols].bitcast(FP8X4),
-                    scales=text_scales[:, cols],
-                    in_=grouped[:].rearrange("p s a j -> p (s a j)"),
+                    out=video_codes[:, cols].bitcast(FP8X4), scales=video_scales[:, cols],
+                    in_=video_grouped[:, values],
                 )
 
-            prepare_text_quad(0)
-            for step in range(-1, TOKENS - 1):
-                if (step + 1) % QUAD == 0 and step + 1 + QUAD < TOKENS:
-                    prepare_text_quad((step + 1) // QUAD + 1)
-                pipeline_step(step)
+            def quantise_texts(batch):
+                first = (batch - first_text) * QUAD * P
+                cols = slice(first, first + QUAD * P)
+                nc.vector.quantize_mx(
+                    out=text_codes[:, cols].bitcast(FP8X4), scales=text_scales[:, cols],
+                    in_=grouped_of[batch][:],
+                )
 
+            for batch in range(batches):
+                load(batch)
+            for slot in range(batches + 3):
+                swept = slot - 3
+                if swept == first_text - 1:
+                    for group in range(GROUPS):
+                        quantise_videos(group)
+                tokens = []
+                if swept >= first_text:
+                    quantise_texts(swept)
+                    first = (swept - first_text) * QUAD
+                    tokens = list(range(first, first + QUAD))
+                for token in tokens[:2]:
+                    multiply(token)
+                if 0 <= slot - 1 < batches:
+                    invert_norms(slot - 1)
+                    normalise(slot - 1)
+                if 0 <= slot - 2 < batches:
+                    turn(slot - 2)
+                if slot < batches:
+                    add_up_squares(slot)
+                for token in tokens:
+                    raise_top(token)
+                    if token + 2 in tokens:
+                        multiply(token + 2)
+            multiply(TOKENS)
+            finish_top(TOKENS - 1)
+
+        quad_work = pools.enter_context(tc.tile_pool(name="quad_work", bufs=3))
+        token_work = pools.enter_context(tc.tile_pool(name="token_work", bufs=4))
         finish = pools.enter_context(tc.tile_pool(name="finish", bufs=4))
 
         def turn_top_pieces(group):
             made = {}
 
             def repeat():
-                made["repeated"] = finish.tile([P, QUAD, GROUP_VIDEOS], F32, tag="repeated", name="repeated", bufs=2)
+                made["repeated"] = finish.tile([P, QUAD, GROUP_VIDEOS], F32, tag="repeated", name="repeated")
                 nc.scalar.copy(
                     out=made["repeated"][:],
                     in_=top[:, group_videos(group)].unsqueeze(1).to_broadcast([P, QUAD, GROUP_VIDEOS]),
                 )
 
             def turn():
-                made["bank"] = psum.tile([P, P], F32, tag="turned", name="turned_top", bufs=1)
+                bank = psum.tile([P, P], F32, tag="turned", name="turned_top", bufs=1)
                 nc.tensor.transpose(
-                    made["bank"][:], made["repeated"][:].rearrange("a s b -> a (s b)"), ident_f32[:]
+                    bank[:], made["repeated"][:].rearrange("a s b -> a (s b)"), ident_f32[:]
                 )
+                nc.scalar.copy(out=top_turned[:, group, :], in_=bank[:])
 
-            def keep_turned():
-                nc.scalar.copy(out=top_turned[:, group, :], in_=made["bank"][:])
+            return [repeat, turn]
 
-            return [repeat, turn, keep_turned]
+        def turn_products(group):
+            bank = psum.tile([P, BLOCKS, P], F32, tag="turned", name="turned_products", bufs=1)
+            columns = product_sums[group][:].rearrange("a v b -> a (v b)")
+            for k in range(BLOCKS):
+                nc.tensor.transpose(bank[:, k, :], columns[:, k * P : (k + 1) * P], ident_f32[:])
+            store(group, 1, unit_blocks(TOKEN_UNIT), bank[:])
 
-        def product_sum_pieces(group):
-            made = {}
+        def take_logarithms(group):
+            nc.scalar.activation(
+                out=sums[:, group, 0, :, :], in_=sums[:, group, 0, :, :], func=FN.Ln
+            )
 
-            def turn():
-                made["bank"] = psum.tile([P, BLOCKS, P], F32, tag="turned", name="turned_products", bufs=1)
-                columns = product_sums[group][:].rearrange("a v b -> a (v b)")
-                for k in range(BLOCKS):
-                    nc.tensor.transpose(
-                        made["bank"][:, k, :], columns[:, k * P : (k + 1) * P], ident_f32[:]
-                    )
+        def invert_logarithms(group, unit):
+            weights = sums[:, group, 0, unit_blocks(unit), :]
+            nc.scalar.activation(out=weights, in_=weights, func=FN.Exp, scale=-1.0)
 
-            def keep_turned():
-                store(token_sums[group], 1, slice(0, BLOCKS), made["bank"][:])
+        def invert_block(group, block):
+            weights = sums[:, group, 0, block, :]
+            nc.vector.reciprocal(out=weights, in_=weights)
 
-            return [turn, keep_turned]
-
-        def pooling_pieces(sums, group, entry):
-            made = {}
-
-            def invert():
-                made["weights"] = sums()[:, 0, :, :]
-                made["means"] = sums()[:, 1, :, :]
-                nc.scalar.activation(out=made["weights"], in_=made["weights"], func=FN.Ln)
-
-            def invert_more():
-                nc.scalar.activation(out=made["weights"], in_=made["weights"], func=FN.Exp, scale=-1.0)
+        def pooling_pieces(group, unit):
+            weights = sums[:, group, 0, unit_blocks(unit), :]
+            means = sums[:, group, 1, unit_blocks(unit), :]
 
             def divide():
-                nc.gpsimd.tensor_tensor(
-                    out=made["means"], in0=made["means"], in1=made["weights"], op=ALU.mult
-                )
+                nc.gpsimd.tensor_tensor(out=means, in0=means, in1=weights, op=ALU.mult)
 
             def deviate():
                 nc.vector.tensor_tensor(
-                    out=made["means"], in0=made["means"],
+                    out=means, in0=means,
                     in1=top_turned[:, group, :].unsqueeze(1).to_broadcast([P, BLOCKS, P]),
                     op=ALU.subtract,
                 )
 
             def weigh_means():
-                nc.scalar.activation(
-                    out=made["weights"], in_=made["means"], func=FN.Exp, scale=sharp_top[:, 0:1]
-                )
+                nc.scalar.activation(out=weights, in_=means, func=FN.Exp, scale=sharp_top[:, 0:1])
 
             def form_products():
-                nc.gpsimd.tensor_tensor(
-                    out=made["means"], in0=made["means"], in1=made["weights"], op=ALU.mult
-                )
+                nc.gpsimd.tensor_tensor(out=means, in0=means, in1=weights, op=ALU.mult)
 
             def turn_back():
                 bank = psum.tile([P, 2, QUAD, GROUP_VIDEOS], F32, tag="turned", name="turned_back", bufs=1)
@@ -474,39 +489,64 @@ def tile_mug_head_kernel(tc, text_feat, video_feat, text_mask, out):
                     for k in range(BLOCKS):
                         transpose_add(
                             bank[:, plane, :, :].rearrange("a s b -> a (s b)"),
-                            sums()[:, plane, k, :],
+                            sums[:, group, plane, unit * BLOCKS + k, :],
                             k == 0,
                             k == BLOCKS - 1,
                         )
                 nc.vector.tensor_reduce(
-                    out=statistics[:, entry, :, group_videos(group)],
+                    out=statistics[:, unit, :, group_videos(group)],
                     in_=bank[:].rearrange("a q s b -> a q b s"),
                     axis=INNERMOST,
                     op=ALU.add,
                 )
 
-            return [invert, invert_more, divide, deviate, weigh_means, form_products, turn_back]
+            return [divide, deviate, weigh_means, form_products, turn_back]
 
+        def woven(chains):
+            pieces = []
+            for slot in range(len(chains) + max(len(chain) for chain in chains)):
+                for number, chain in enumerate(chains):
+                    if 0 <= slot - number < len(chain):
+                        pieces.append(chain[slot - number])
+            return pieces
+
+        last = GROUPS - 1
         waiting = []
         for group in range(GROUPS):
             first_step = (group + 1) * TOKENS
             for piece in turn_top_pieces(group):
                 waiting.append((first_step, piece))
-            half_done = first_step + HALF + FRAME_LAG
-            for piece in pooling_pieces(lambda group=group: frame_sums[group, 0], group, 0):
-                waiting.append((half_done, piece))
-            all_done = first_step + TOKENS + FRAME_LAG
-            for piece in product_sum_pieces(group):
-                waiting.append((all_done, piece))
-            by_tokens = pooling_pieces(lambda group=group: frame_sums[group, 1], group, 1)
-            by_frames = pooling_pieces(lambda group=group: token_sums[group], group, 2)
-            for pair in zip(by_tokens, by_frames):
-                for piece in pair:
-                    waiting.append((all_done, piece))
+            if group < last:
+                waiting.append((first_step + TOKENS, lambda group=group: turn_products(group)))
+        stored = FIRST_STEPS + FRAME_LAG
+        for group in range(last):
+            waiting.append((stored, lambda group=group: take_logarithms(group)))
+        chains = []
+        for group in range(last):
+            for unit in range(UNITS):
+                invert = lambda group=group, unit=unit: invert_logarithms(group, unit)
+                chains.append([invert] + pooling_pieces(group, unit))
+        for piece in woven(chains):
+            waiting.append((stored, piece))
+        def wait_for_block(block, stored):
+            waiting.append((stored, lambda: invert_block(last, block)))
+
+        for quad in range(QUADS):
+            if quad == QUADS - 1:
+                waiting.append((STEPS + 1, lambda: turn_products(last)))
+                for block in range(QUADS, UNITS * BLOCKS):
+                    wait_for_block(block, STEPS + 1)
+            stored = FIRST_STEPS + (quad + 1) * QUAD + FRAME_LAG
+            wait_for_block(quad, stored)
+            if quad == BLOCKS - 1:
+                for piece in pooling_pieces(last, 0):
+                    waiting.append((stored, piece))
+        for piece in woven([pooling_pieces(last, 1), pooling_pieces(last, TOKEN_UNIT)]):
+            waiting.append((STEPS + FRAME_LAG, piece))
 
         with tc.manual_schedule():
             served = 0
-            for step in range(TOKENS - 1, STEPS + FRAME_LAG + 1):
+            for step in range(TOKENS, STEPS + FRAME_LAG + 1):
                 pipeline_step(step)
                 for turn in range(PIECES_PER_STEP):
                     if served < len(waiting) and waiting[served][0] <= step:

@@ -36,7 +36,7 @@ FIRST_STEPS = GROUPS * TOKENS
 STEPS = FIRST_STEPS + TOKENS
 FRAME_LAG = 4
 TOKEN_LAG = 2
-PIECES_PER_STEP = 3
+PIECES_PER_STEP = 2
 
 FLOPS = 2 * (P * TOKENS) * (P * FRAMES) * FEATURES
 
@@ -86,7 +86,7 @@ def tile_mug_head_kernel(tc, text_feat, video_feat, text_mask, out):
                 out=acc, lhsT=block, rhs=ident_f32[:], is_transpose=True, start=start, stop=stop
             )
 
-        group_work = pools.enter_context(tc.tile_pool(name="group_work", bufs=2))
+        group_work = pools.enter_context(tc.tile_pool(name="group_work", bufs=GROUPS))
 
         def similarities(token, group, tag, bufs, times):
             sim = psum.tile([P, GROUP_COLS], F32, tag=tag, name="sim", bufs=bufs)
@@ -255,25 +255,27 @@ def tile_mug_head_kernel(tc, text_feat, video_feat, text_mask, out):
             quad = step // QUAD
             plane = (step % QUAD) // 2
             first_frame = (step % 2) * (FRAMES // 2)
-            if step % QUAD == 0:
-                quad_banks[quad] = psum.tile([P, 2, 1, P], F32, tag="quad_sums", name="quad_sums", bufs=1)
+            if step % 2 == 0:
+                quad_banks[quad, plane] = psum.tile(
+                    [P, 1, P], F32, tag="quad_sums%d" % plane, name="quad_sums", bufs=1
+                )
             for v in range(first_frame, first_frame + FRAMES // 2):
                 transpose_add(
-                    quad_banks[quad][:, plane, 0, :],
+                    quad_banks[quad, plane][:, 0, :],
                     quad_tiles[quad][plane][:, v, :, :].rearrange("a s b -> a (s b)"),
                     v == 0,
                     v == FRAMES - 1,
                 )
 
         def store_frame_sums(step):
-            if not in_second_sweep(step) or step % QUAD != QUAD - 1:
+            if not in_second_sweep(step) or step % 2 == 0:
                 return
             block = step % TOKENS // QUAD
-            for plane in range(2):
-                store(
-                    step // TOKENS - 1, plane, slice(block, block + 1),
-                    quad_banks[step // QUAD][:, plane, :, :],
-                )
+            plane = (step % QUAD) // 2
+            store(
+                step // TOKENS - 1, plane, slice(block, block + 1),
+                quad_banks[step // QUAD, plane][:],
+            )
 
         def pipeline_step(step):
             multiply(step + 1)
@@ -409,10 +411,10 @@ def tile_mug_head_kernel(tc, text_feat, video_feat, text_mask, out):
                 if 0 <= slot - 1 < batches:
                     invert_norms(slot - 1)
                     normalise(slot - 1)
-                if 0 <= slot - 2 < batches:
-                    turn(slot - 2)
                 if slot < batches:
                     add_up_squares(slot)
+                if 0 <= slot - 2 < batches:
+                    turn(slot - 2)
                 for token in tokens:
                     raise_top(token)
                     if token + 2 in tokens:
@@ -424,6 +426,16 @@ def tile_mug_head_kernel(tc, text_feat, video_feat, text_mask, out):
         token_work = pools.enter_context(tc.tile_pool(name="token_work", bufs=4))
         finish = pools.enter_context(tc.tile_pool(name="finish", bufs=4))
 
+        last = GROUPS - 1
+
+        def plain(work):
+            return (False, work)
+
+        def turning(work):
+            return (True, work)
+
+        result = finish.tile([P, P], F32, name="result", bufs=1)
+
         def turn_top_pieces(group):
             made = {}
 
@@ -434,57 +446,65 @@ def tile_mug_head_kernel(tc, text_feat, video_feat, text_mask, out):
                     in_=top[:, group_videos(group)].unsqueeze(1).to_broadcast([P, QUAD, GROUP_VIDEOS]),
                 )
 
-            def turn():
-                bank = psum.tile([P, P], F32, tag="turned", name="turned_top", bufs=1)
+            def turn(tag, bufs):
+                bank = psum.tile([P, P], F32, tag=tag, name="turned_top", bufs=bufs)
                 nc.tensor.transpose(
                     bank[:], made["repeated"][:].rearrange("a s b -> a (s b)"), ident_f32[:]
                 )
-                nc.scalar.copy(out=top_turned[:, group, :], in_=bank[:])
+                return lambda: nc.scalar.copy(out=top_turned[:, group, :], in_=bank[:])
 
-            return [repeat, turn]
+            return [plain(repeat), turning(turn)]
 
-        def turn_products(group):
-            bank = psum.tile([P, BLOCKS, P], F32, tag="turned", name="turned_products", bufs=1)
-            columns = product_sums[group][:].rearrange("a v b -> a (v b)")
-            for k in range(BLOCKS):
-                nc.tensor.transpose(bank[:, k, :], columns[:, k * P : (k + 1) * P], ident_f32[:])
-            store(group, 1, unit_blocks(TOKEN_UNIT), bank[:])
+        def turn_product_pieces(group):
+            def turn(tag, bufs):
+                bank = psum.tile([P, BLOCKS, P], F32, tag=tag, name="turned_products", bufs=bufs)
+                columns = product_sums[group][:].rearrange("a v b -> a (v b)")
+                for k in range(BLOCKS):
+                    nc.tensor.transpose(bank[:, k, :], columns[:, k * P : (k + 1) * P], ident_f32[:])
+                return lambda: store(group, 1, unit_blocks(TOKEN_UNIT), bank[:])
 
-        def take_logarithms(group):
-            nc.scalar.activation(
-                out=sums[:, group, 0, :, :], in_=sums[:, group, 0, :, :], func=FN.Ln
-            )
+            return [turning(turn)]
 
-        def invert_logarithms(group, unit):
-            weights = sums[:, group, 0, unit_blocks(unit), :]
+        def take_logarithms(groups):
+            for group in groups:
+                weights = sums[:, group, 0, :, :]
+                nc.scalar.activation(out=weights, in_=weights, func=FN.Ln)
+
+        def invert_logarithms(group, blocks):
+            weights = sums[:, group, 0, blocks, :]
             nc.scalar.activation(out=weights, in_=weights, func=FN.Exp, scale=-1.0)
 
         def invert_block(group, block):
             weights = sums[:, group, 0, block, :]
             nc.vector.reciprocal(out=weights, in_=weights)
 
-        def pooling_pieces(group, unit):
-            weights = sums[:, group, 0, unit_blocks(unit), :]
-            means = sums[:, group, 1, unit_blocks(unit), :]
+        def weighing_pieces(group, blocks, multiply_engine):
+            weights = sums[:, group, 0, blocks, :]
+            means = sums[:, group, 1, blocks, :]
 
             def divide():
-                nc.gpsimd.tensor_tensor(out=means, in0=means, in1=weights, op=ALU.mult)
+                multiply_engine.tensor_tensor(out=means, in0=means, in1=weights, op=ALU.mult)
 
             def deviate():
+                tops = top_turned[:, group, :].unsqueeze(1)
                 nc.vector.tensor_tensor(
                     out=means, in0=means,
-                    in1=top_turned[:, group, :].unsqueeze(1).to_broadcast([P, BLOCKS, P]),
-                    op=ALU.subtract,
+                    in1=tops.to_broadcast([P, blocks.stop - blocks.start, P]), op=ALU.subtract,
                 )
 
             def weigh_means():
                 nc.scalar.activation(out=weights, in_=means, func=FN.Exp, scale=sharp_top[:, 0:1])
 
             def form_products():
-                nc.gpsimd.tensor_tensor(out=means, in0=means, in1=weights, op=ALU.mult)
+                multiply_engine.tensor_tensor(out=means, in0=means, in1=weights, op=ALU.mult)
 
-            def turn_back():
-                bank = psum.tile([P, 2, QUAD, GROUP_VIDEOS], F32, tag="turned", name="turned_back", bufs=1)
+            return [plain(divide), plain(deviate), plain(weigh_means), plain(form_products)]
+
+        def adding_pieces(group, unit):
+            def turn_back(tag, bufs):
+                bank = psum.tile(
+                    [P, 2, QUAD, GROUP_VIDEOS], F32, tag=tag, name="turned_back", bufs=bufs
+                )
                 for plane in range(2):
                     for k in range(BLOCKS):
                         transpose_add(
@@ -493,14 +513,49 @@ def tile_mug_head_kernel(tc, text_feat, video_feat, text_mask, out):
                             k == 0,
                             k == BLOCKS - 1,
                         )
-                nc.vector.tensor_reduce(
+                return lambda: nc.vector.tensor_reduce(
                     out=statistics[:, unit, :, group_videos(group)],
                     in_=bank[:].rearrange("a q s b -> a q b s"),
                     axis=INNERMOST,
                     op=ALU.add,
                 )
 
-            return [divide, deviate, weigh_means, form_products, turn_back]
+            return [turning(turn_back)]
+
+        def result_pieces(group):
+            videos = group_videos(group)
+
+            def join_halves():
+                halves = statistics[:, 0, :, videos]
+                nc.vector.tensor_tensor(
+                    out=halves, in0=halves, in1=statistics[:, 1, :, videos], op=ALU.add
+                )
+
+            def divide():
+                for unit in (0, TOKEN_UNIT):
+                    weights = statistics[:, unit, 0, videos]
+                    nc.vector.reciprocal(out=weights, in_=weights)
+                for unit in (0, TOKEN_UNIT):
+                    products = statistics[:, unit, 1, videos]
+                    nc.vector.tensor_tensor(
+                        out=products, in0=products, in1=statistics[:, unit, 0, videos], op=ALU.mult
+                    )
+
+            def put_out():
+                nc.vector.tensor_tensor(
+                    out=result[:, videos], in0=statistics[:, 0, 1, videos],
+                    in1=statistics[:, TOKEN_UNIT, 1, videos], op=ALU.add,
+                )
+                nc.vector.scalar_tensor_tensor(
+                    out=result[:, videos], in0=result[:, videos], scalar=0.5, in1=top[:, videos],
+                    op0=ALU.mult, op1=ALU.add,
+                )
+                nc.vector.tensor_scalar_mul(
+                    out=result[:, videos], in0=result[:, videos], scalar1=mask_top[:, 0:1]
+                )
+                nc.sync.dma_start(out=out[:, videos], in_=result[:, videos])
+
+            return [plain(join_halves), plain(divide), plain(put_out)]
 
         def woven(chains):
             pieces = []
@@ -510,66 +565,91 @@ def tile_mug_head_kernel(tc, text_feat, video_feat, text_mask, out):
                         pieces.append(chain[slot - number])
             return pieces
 
-        last = GROUPS - 1
-        waiting = []
-        for group in range(GROUPS):
-            first_step = (group + 1) * TOKENS
-            for piece in turn_top_pieces(group):
-                waiting.append((first_step, piece))
-            if group < last:
-                waiting.append((first_step + TOKENS, lambda group=group: turn_products(group)))
-        stored = FIRST_STEPS + FRAME_LAG
-        for group in range(last):
-            waiting.append((stored, lambda group=group: take_logarithms(group)))
-        chains = []
-        for group in range(last):
-            for unit in range(UNITS):
-                invert = lambda group=group, unit=unit: invert_logarithms(group, unit)
-                chains.append([invert] + pooling_pieces(group, unit))
-        for piece in woven(chains):
-            waiting.append((stored, piece))
-        def wait_for_block(block, stored):
-            waiting.append((stored, lambda: invert_block(last, block)))
+        queues = ([], [], [])
 
-        for quad in range(QUADS):
-            if quad == QUADS - 1:
-                waiting.append((STEPS + 1, lambda: turn_products(last)))
-                for block in range(QUADS, UNITS * BLOCKS):
-                    wait_for_block(block, STEPS + 1)
-            stored = FIRST_STEPS + (quad + 1) * QUAD + FRAME_LAG
-            wait_for_block(quad, stored)
+        def wait_for(number, step, pieces):
+            queues[number].extend([(step, piece) for piece in pieces])
+
+        def group_chains(groups):
+            chains = []
+            for group in groups:
+                for unit in range(UNITS):
+                    blocks = unit_blocks(unit)
+                    invert = plain(lambda group=group, blocks=blocks: invert_logarithms(group, blocks))
+                    weighing = weighing_pieces(group, blocks, nc.gpsimd)
+                    chains.append([invert] + weighing + adding_pieces(group, unit))
+            return chains
+
+        for number, groups in enumerate((list(range(last - 1)), [last - 1])):
+            swept = (groups[-1] + 2) * TOKENS
+            stored = swept + FRAME_LAG
+            wait_for(number, swept, woven([turn_top_pieces(group) for group in groups]))
+            wait_for(number, swept, woven([turn_product_pieces(group) for group in groups]))
+            wait_for(number, stored, [plain(lambda groups=groups: take_logarithms(groups))])
+            wait_for(number, stored, woven(group_chains(groups)))
+            for group in groups:
+                wait_for(number, stored, result_pieces(group))
+
+        def quad_stored(quad):
+            return FIRST_STEPS + (quad + 1) * QUAD + FRAME_LAG
+
+        def inversions(blocks):
+            return [plain(lambda block=block: invert_block(last, block)) for block in blocks]
+
+        wait_for(2, FIRST_STEPS, turn_top_pieces(last))
+        for quad in range(QUADS - 1):
+            wait_for(2, quad_stored(quad), inversions([quad]))
             if quad == BLOCKS - 1:
-                for piece in pooling_pieces(last, 0):
-                    waiting.append((stored, piece))
-        for piece in woven([pooling_pieces(last, 1), pooling_pieces(last, TOKEN_UNIT)]):
-            waiting.append((STEPS + FRAME_LAG, piece))
+                wait_for(2, quad_stored(quad), weighing_pieces(last, unit_blocks(0), nc.gpsimd))
+                wait_for(2, quad_stored(quad), adding_pieces(last, 0))
+        early = weighing_pieces(last, slice(BLOCKS, QUADS - 1), nc.gpsimd)
+        columns = unit_blocks(TOKEN_UNIT)
+        wait_for(2, quad_stored(QUADS - 2), early[:2])
+        wait_for(2, STEPS + 1, inversions(range(QUADS, QUADS + 2)))
+        wait_for(2, STEPS + 1, early[2:])
+        wait_for(2, STEPS + FRAME_LAG - 1, turn_product_pieces(last))
+        wait_for(2, STEPS + FRAME_LAG - 1, inversions([QUADS - 1]))
+        wait_for(2, STEPS + FRAME_LAG, inversions(range(QUADS + 2, UNITS * BLOCKS)))
+        wait_for(2, STEPS + FRAME_LAG, woven([
+            weighing_pieces(last, slice(QUADS - 1, QUADS), nc.vector) + adding_pieces(last, 1),
+            weighing_pieces(last, columns, nc.vector) + adding_pieces(last, TOKEN_UNIT),
+        ]))
+        wait_for(2, STEPS + FRAME_LAG, result_pieces(last))
+
+        readers = []
+
+        def serve(queue, tag, bufs):
+            turns, work = queue[0][1]
+            queue.remove(queue[0])
+            if turns:
+                readers.append(work(tag, bufs))
+            else:
+                work()
+
+        def read_turned():
+            for reader in readers:
+                reader()
+            readers.clear()
 
         with tc.manual_schedule():
-            served = 0
             for step in range(TOKENS, STEPS + FRAME_LAG + 1):
                 pipeline_step(step)
-                for turn in range(PIECES_PER_STEP):
-                    if served < len(waiting) and waiting[served][0] <= step:
-                        waiting[served][1]()
-                        served += 1
-            for ready, piece in waiting[served:]:
-                piece()
-
-            over_tokens = statistics[:, 0, :, :]
-            nc.vector.tensor_tensor(
-                out=over_tokens, in0=over_tokens, in1=statistics[:, 1, :, :], op=ALU.add
-            )
-            result = finish.tile([P, 2, P], F32, name="result", bufs=1)
-            for part, entry in enumerate((0, 2)):
-                nc.vector.reciprocal(out=result[:, part, :], in_=statistics[:, entry, 0, :])
-                nc.vector.tensor_tensor(
-                    out=result[:, part, :], in0=result[:, part, :], in1=statistics[:, entry, 1, :],
-                    op=ALU.mult,
-                )
-            total = result[:, 0, :]
-            nc.vector.tensor_tensor(out=total, in0=total, in1=result[:, 1, :], op=ALU.add)
-            nc.vector.scalar_tensor_tensor(
-                out=total, in0=total, scalar=0.5, in1=top[:], op0=ALU.mult, op1=ALU.add
-            )
-            nc.vector.tensor_scalar_mul(out=total, in0=total, scalar1=mask_top[:, 0:1])
-            nc.sync.dma_start(out=out, in_=total)
+                read_turned()
+                sweeping = step < FIRST_STEPS
+                tag = "quad_sums%d" % (1 - (step - FRAME_LAG) % QUAD // 2) if sweeping else "first"
+                for number, most in enumerate((PIECES_PER_STEP, PIECES_PER_STEP, 1)):
+                    queue = queues[number]
+                    for turn in range(most):
+                        if not queue or queue[0][0] > step:
+                            break
+                        turns = queue[0][1][0]
+                        if turns and (readers if sweeping or number < 2 else len(readers) > 1):
+                            break
+                        if turns and sweeping and step % 2 == 1:
+                            break
+                        serve(queue, tag, 1 if sweeping else 2)
+            for queue in queues:
+                while queue:
+                    serve(queue, "first", 2)
+                    if len(readers) > 1 or not queue or not queue[0][1][0]:
+                        read_turned()

@@ -34,6 +34,7 @@ TOKEN_UNIT = UNITS - 1
 
 FIRST_STEPS = GROUPS * TOKENS
 STEPS = FIRST_STEPS + TOKENS
+SECOND_LEVEL = FIRST_STEPS - TOKENS
 FRAME_LAG = 4
 TOKEN_LAG = 2
 PIECES_PER_STEP = 2
@@ -109,6 +110,7 @@ def tile_mug_head_kernel(tc, text_feat, video_feat, text_mask, out):
         running_top = {}
         deviations = {}
         weights = {}
+        weight_sums = {}
         quad_tiles = {}
         product_sums = {}
         quad_banks = {}
@@ -119,6 +121,9 @@ def tile_mug_head_kernel(tc, text_feat, video_feat, text_mask, out):
 
         def in_second_sweep(step):
             return TOKENS <= step < STEPS
+
+        def weighed_by_gpsimd(step):
+            return step < SECOND_LEVEL and step % QUAD == 1 and step % TOKENS < TOKENS - QUAD
 
         def group_videos(group):
             return slice(group * GROUP_VIDEOS, (group + 1) * GROUP_VIDEOS)
@@ -143,22 +148,23 @@ def tile_mug_head_kernel(tc, text_feat, video_feat, text_mask, out):
                 op=ALU.subtract,
             )
 
-        def raise_top(step):
+        def raise_top(step, strand=0):
             if not in_first_sweep(step):
                 return
             token = step % TOKENS
             group = step // TOKENS
             bar = barred[:, token : token + 1]
-            if token == 0:
-                running_top[group] = group_work.tile([P, GROUP_COLS], F32, tag="running", name="running")
+            if (group, strand) not in running_top:
+                running = group_work.tile([P, GROUP_COLS], F32, tag="running", name="running")
+                running_top[group, strand] = running
                 nc.vector.tensor_scalar(
-                    out=running_top[group][:], in0=sim_first[step][:], scalar1=bar, scalar2=None,
-                    op0=ALU.add,
+                    out=running[:], in0=sim_first[step][:], scalar1=bar, scalar2=None, op0=ALU.add
                 )
             else:
+                running = running_top[group, strand]
                 nc.vector.scalar_tensor_tensor(
-                    out=running_top[group][:], in0=sim_first[step][:], scalar=bar,
-                    in1=running_top[group][:], op0=ALU.add, op1=ALU.max,
+                    out=running[:], in0=sim_first[step][:], scalar=bar, in1=running[:],
+                    op0=ALU.add, op1=ALU.max,
                 )
 
         def finish_top(step):
@@ -166,7 +172,7 @@ def tile_mug_head_kernel(tc, text_feat, video_feat, text_mask, out):
                 group = step // TOKENS
                 nc.vector.tensor_reduce(
                     out=top[:, group_videos(group)],
-                    in_=running_top[group][:].rearrange("a (v b) -> a b v", v=FRAMES),
+                    in_=running_top[group, 0][:].rearrange("a (v b) -> a b v", v=FRAMES),
                     axis=INNERMOST,
                     op=ALU.max,
                 )
@@ -181,15 +187,16 @@ def tile_mug_head_kernel(tc, text_feat, video_feat, text_mask, out):
                     quad_work.tile(quad_shape, F32, tag="quad_weights", name="quad_weights"),
                     quad_work.tile(quad_shape, F32, tag="quad_products", name="quad_products"),
                 )
-            weights[step] = token_work.tile([P, GROUP_COLS], F32, tag="weight", name="weight")
-            by_frame = "a (v b) -> a v b"
-            for target, source in (
-                (weights[step][:], deviations[step][:]),
+            targets = [
                 (
                     quad_tiles[step // QUAD][0][:, :, step % QUAD, :],
-                    deviations[step][:].rearrange(by_frame, v=FRAMES),
-                ),
-            ):
+                    deviations[step][:].rearrange("a (v b) -> a v b", v=FRAMES),
+                )
+            ]
+            if not weighed_by_gpsimd(step):
+                weights[step] = token_work.tile([P, GROUP_COLS], F32, tag="weight", name="weight")
+                targets.append((weights[step][:], deviations[step][:]))
+            for target, source in targets:
                 nc.scalar.activation(
                     out=target, in_=source, func=FN.Exp,
                     scale=sharp_mask[:, token : token + 1], bias=barred[:, token : token + 1],
@@ -201,7 +208,7 @@ def tile_mug_head_kernel(tc, text_feat, video_feat, text_mask, out):
             nc.vector.tensor_tensor(
                 out=quad_tiles[step // QUAD][1][:, :, step % QUAD, :],
                 in0=sim_second[step][:].rearrange("a (v b) -> a v b", v=FRAMES),
-                in1=weights[step][:].rearrange("a (v b) -> a v b", v=FRAMES),
+                in1=quad_tiles[step // QUAD][0][:, :, step % QUAD, :],
                 op=ALU.mult,
             )
 
@@ -221,22 +228,43 @@ def tile_mug_head_kernel(tc, text_feat, video_feat, text_mask, out):
                 out=acc[:], in0=so_far, in1=products[:, :, step % QUAD, :], op=ALU.add
             )
 
+        def add_up_gpsimd_weights(step):
+            if not in_second_sweep(step) or not weighed_by_gpsimd(step):
+                return
+            group = step // TOKENS - 1
+            terms = quad_tiles[step // QUAD][0][:, :, step % QUAD, :]
+            if step % TOKENS == 1:
+                weight_sums[group] = group_work.tile(
+                    [P, FRAMES, GROUP_VIDEOS], F32, tag="weight_sums", name="weight_sums"
+                )
+                nc.gpsimd.tensor_scalar(
+                    out=weight_sums[group][:], in0=terms, scalar1=1.0, scalar2=0.0,
+                    op0=ALU.mult, op1=ALU.add,
+                )
+            else:
+                acc = weight_sums[group]
+                nc.gpsimd.tensor_tensor(out=acc[:], in0=acc[:], in1=terms, op=ALU.add)
+
         def add_up_weights(step):
-            if not in_second_sweep(step):
+            if not in_second_sweep(step) or weighed_by_gpsimd(step):
                 return
             token = step % TOKENS
             group = step // TOKENS - 1
+            shares = [weights[step][:]]
+            if token == TOKENS - QUAD + 1 and group in weight_sums:
+                shares.append(weight_sums[group][:].rearrange("a v b -> a (v b)"))
             if token == 0:
                 weight_banks[group] = psum.tile(
                     [P, BLOCKS, P], F32, tag="weight_sums", name="weight_sums", bufs=1
                 )
-            for k in range(BLOCKS):
-                transpose_add(
-                    weight_banks[group][:, k, :],
-                    weights[step][:, k * P : (k + 1) * P],
-                    token == 0 and k == 0,
-                    token == TOKENS - 1 and k == BLOCKS - 1,
-                )
+            for terms in shares:
+                for k in range(BLOCKS):
+                    transpose_add(
+                        weight_banks[group][:, k, :],
+                        terms[:, k * P : (k + 1) * P],
+                        token == 0 and k == 0,
+                        token == TOKENS - 1 and k == BLOCKS - 1,
+                    )
             if token == TOKENS - 1:
                 store(group, 0, unit_blocks(TOKEN_UNIT), weight_banks[group][:])
 
@@ -286,6 +314,7 @@ def tile_mug_head_kernel(tc, text_feat, video_feat, text_mask, out):
             form_product(step - 1)
             finish_top(step)
             add_up_products(step - 1)
+            add_up_gpsimd_weights(step - 1)
             add_up_weights(step - TOKEN_LAG)
             add_up_frames(step - FRAME_LAG)
 
@@ -294,6 +323,7 @@ def tile_mug_head_kernel(tc, text_feat, video_feat, text_mask, out):
         rows_of = {}
         squares_of = {}
         normal_of = {}
+        turned_of = {}
         grouped_of = {}
 
         with tc.manual_schedule(), tc.tile_pool(name="prep", bufs=3) as prep:
@@ -313,56 +343,51 @@ def tile_mug_head_kernel(tc, text_feat, video_feat, text_mask, out):
                     source = text_feat[:, first : first + QUAD, :]
                 nc.sync.dma_start(out=rows_of[batch][:], in_=source)
 
-            def add_up_squares(batch):
-                sums_of_squares = prep.tile([P, QUAD], F32, tag="squares", name="sums_of_squares")
-                squares_of[batch] = sums_of_squares
-                for i in range(QUAD):
-                    row = rows_of[batch][:, i, :]
-                    total = sums_of_squares[:, i : i + 1]
-                    if i % 2 == 0 or batch >= first_text + BLOCKS - 1:
-                        scratch = prep.tile([P, FEATURES], BF16, tag="scratch_s", name="scratch_s")
-                        nc.scalar.activation(out=scratch[:], in_=row, func=FN.Square, accum_out=total)
-                    else:
-                        scratch = prep.tile([P, FEATURES], BF16, tag="scratch_v", name="scratch_v")
-                        nc.vector.scalar_tensor_tensor(
-                            out=scratch[:], in0=row, scalar=1.0, in1=row,
-                            op0=ALU.mult, op1=ALU.mult, accum_out=total,
-                        )
+            def squares_on_vector(batch):
+                return [] if batch >= first_text + BLOCKS - 1 else [1, 3]
 
-            def invert_norms(batch):
-                norms = squares_of[batch]
-                nc.scalar.sqrt(out=norms[:], in_=norms[:])
-                nc.vector.tensor_scalar_max(out=norms[:], in0=norms[:], scalar1=EPS)
-                nc.vector.reciprocal(out=norms[:], in_=norms[:])
+            def add_up_squares(batch, i):
+                if batch not in squares_of:
+                    squares_of[batch] = prep.tile([P, QUAD], F32, tag="squares", name="squares")
+                row = rows_of[batch][:, i, :]
+                total = squares_of[batch][:, i : i + 1]
+                if i in squares_on_vector(batch):
+                    scratch = prep.tile([P, FEATURES], BF16, tag="scratch_v", name="scratch_v")
+                    nc.vector.scalar_tensor_tensor(
+                        out=scratch[:], in0=row, scalar=1.0, in1=row,
+                        op0=ALU.mult, op1=ALU.mult, accum_out=total,
+                    )
+                else:
+                    scratch = prep.tile([P, FEATURES], BF16, tag="scratch_s", name="scratch_s")
+                    nc.scalar.activation(out=scratch[:], in_=row, func=FN.Square, accum_out=total)
 
             def normalise(batch):
                 normal = prep.tile([P, QUAD, FEATURES], BF16, tag="normal", name="normal")
                 normal_of[batch] = normal
                 for i in range(QUAD):
                     inverse = squares_of[batch][:, i : i + 1]
-                    if batch < first_text:
-                        nc.vector.tensor_scalar_mul(
-                            out=normal[:, i, :], in0=rows_of[batch][:, i, :], scalar1=inverse
-                        )
-                    else:
-                        nc.gpsimd.tensor_scalar(
-                            out=normal[:, i, :], in0=rows_of[batch][:, i, :],
-                            scalar1=inverse, scalar2=0.0, op0=ALU.mult, op1=ALU.add,
-                        )
+                    nc.vector.tensor_scalar_mul(
+                        out=normal[:, i, :], in0=rows_of[batch][:, i, :], scalar1=inverse
+                    )
 
             def turn(batch):
-                if batch >= first_text:
-                    grouped_of[batch] = prep.tile(
-                        [P, QUAD * P * PACK], BF16, tag="text_grouped", name="text_grouped", align_bytes=64
-                    )
                 for pair in range(0, QUAD, 2):
                     bank = psum.tile([P, 2, 2, P], F32, tag="second", name="turned_rows", bufs=3)
+                    turned_of[batch, pair] = bank
                     for i in range(2):
                         words = normal_of[batch][:, pair + i, :].bitcast(F32)
                         for u in range(2):
                             nc.tensor.transpose(
                                 bank[:, i, u, :], words[:, u : FEATURES // 2 : 2], ident_f32[:]
                             )
+
+            def take_out(batch):
+                if batch >= first_text:
+                    grouped_of[batch] = prep.tile(
+                        [P, QUAD * P * PACK], BF16, tag="text_grouped", name="text_grouped", align_bytes=64
+                    )
+                for pair in range(0, QUAD, 2):
+                    bank = turned_of[batch, pair]
                     if batch >= first_text:
                         target = grouped_of[batch][:].bitcast(F32)
                         nc.scalar.copy(
@@ -396,29 +421,51 @@ def tile_mug_head_kernel(tc, text_feat, video_feat, text_mask, out):
 
             for batch in range(batches):
                 load(batch)
-            for slot in range(batches + 3):
+            left_over = []
+            for slot in range(batches + 4):
                 swept = slot - 3
+                if 0 <= slot - 2 < batches:
+                    turn(slot - 2)
                 if swept == first_text - 1:
                     for group in range(GROUPS):
                         quantise_videos(group)
                 tokens = []
-                if swept >= first_text:
+                if first_text <= swept < batches:
                     quantise_texts(swept)
                     first = (swept - first_text) * QUAD
                     tokens = list(range(first, first + QUAD))
-                for token in tokens[:2]:
-                    multiply(token)
-                if 0 <= slot - 1 < batches:
-                    invert_norms(slot - 1)
+                for token, tag in zip(tokens, ("first", "first", "quad_sums0", "quad_sums1")):
+                    sim_first[token] = similarities(token, 0, tag, 2 if tag == "first" else 1, 1)
+                fillers = [lambda token=token: raise_top(token, token % 2) for token in left_over]
+                if slot < batches:
+                    fillers.extend([
+                        lambda i=i, slot=slot: add_up_squares(slot, i) for i in squares_on_vector(slot)
+                    ])
+                normalised = 0 <= slot - 1 < batches
+                if normalised:
+                    norms = squares_of[slot - 1]
+                    nc.scalar.sqrt(out=norms[:], in_=norms[:])
+                    nc.vector.tensor_scalar_max(out=norms[:], in0=norms[:], scalar1=EPS)
+                for filler in fillers[:1]:
+                    filler()
+                if normalised:
+                    nc.vector.reciprocal(out=norms[:], in_=norms[:])
+                for filler in fillers[1:]:
+                    filler()
+                if normalised:
                     normalise(slot - 1)
                 if slot < batches:
-                    add_up_squares(slot)
+                    for i in range(QUAD):
+                        if i not in squares_on_vector(slot):
+                            add_up_squares(slot, i)
                 if 0 <= slot - 2 < batches:
-                    turn(slot - 2)
-                for token in tokens:
-                    raise_top(token)
-                    if token + 2 in tokens:
-                        multiply(token + 2)
+                    take_out(slot - 2)
+                for token in tokens[:2]:
+                    raise_top(token, token % 2)
+                left_over = tokens[2:]
+            nc.vector.tensor_tensor(
+                out=running_top[0, 0][:], in0=running_top[0, 0][:], in1=running_top[0, 1][:], op=ALU.max
+            )
             multiply(TOKENS)
             finish_top(TOKENS - 1)
 

@@ -24,6 +24,7 @@ TINY = 1.0e-30
 LOW = -1.0e-20
 
 GROUPS = 4
+LAST = GROUPS - 1
 GROUP_VIDEOS = P // GROUPS
 GROUP_COLS = FRAMES * GROUP_VIDEOS
 BLOCKS = GROUP_COLS // P
@@ -35,6 +36,9 @@ TOKEN_UNIT = UNITS - 1
 FIRST_STEPS = GROUPS * TOKENS
 STEPS = FIRST_STEPS + TOKENS
 SECOND_LEVEL = FIRST_STEPS - TOKENS
+LOG_STEP = SECOND_LEVEL + 7
+CATCH_UP = LOG_STEP + 2
+AHEAD = 6
 FRAME_LAG = 4
 TOKEN_LAG = 2
 PIECES_PER_STEP = 2
@@ -66,12 +70,19 @@ def tile_mug_head_kernel(tc, text_feat, video_feat, text_mask, out):
         nc.vector.tensor_reduce(out=mask_top[:], in_=mask[:], axis=INNERMOST, op=ALU.max)
         sharp_top = consts.tile([P, 1], F32, name="sharp_top")
         nc.vector.tensor_scalar_mul(out=sharp_top[:], in0=mask_top[:], scalar1=TAU)
+        half_mask_top = consts.tile([P, 1], F32, name="half_mask_top")
+        nc.vector.tensor_scalar_mul(out=half_mask_top[:], in0=mask_top[:], scalar1=0.5)
         nudge = consts.tile([P, 2], F32, name="nudge")
         for plane, value in enumerate((TINY, LOW)):
             nc.vector.tensor_scalar(
                 out=nudge[:, plane : plane + 1], in0=mask_top[:], scalar1=0.0, scalar2=value,
                 op0=ALU.mult, op1=ALU.add,
             )
+
+        tiny_block = consts.tile([P, P], F32, name="tiny_block")
+        nc.vector.tensor_scalar(
+            out=tiny_block[:], in0=ident_f32[:], scalar1=0.0, scalar2=TINY, op0=ALU.mult, op1=ALU.add
+        )
 
         text_codes = keep.tile([P, TOKENS * P], U32, name="text_codes", align_bytes=64)
         text_scales = keep.tile([P, TOKENS * P], U8, name="text_scales", align_bytes=64)
@@ -108,6 +119,7 @@ def tile_mug_head_kernel(tc, text_feat, video_feat, text_mask, out):
         sim_first = {}
         sim_second = {}
         running_top = {}
+        frame_tops = {}
         deviations = {}
         weights = {}
         weight_sums = {}
@@ -119,6 +131,15 @@ def tile_mug_head_kernel(tc, text_feat, video_feat, text_mask, out):
         def in_first_sweep(step):
             return 0 <= step < FIRST_STEPS
 
+        def first_sweeps(step):
+            if step < CATCH_UP:
+                steps = [step]
+            elif step == CATCH_UP:
+                steps = list(range(step, step + AHEAD + 1))
+            else:
+                steps = [step + AHEAD]
+            return [first for first in steps if in_first_sweep(first)]
+
         def in_second_sweep(step):
             return TOKENS <= step < STEPS
 
@@ -128,13 +149,17 @@ def tile_mug_head_kernel(tc, text_feat, video_feat, text_mask, out):
         def group_videos(group):
             return slice(group * GROUP_VIDEOS, (group + 1) * GROUP_VIDEOS)
 
+        def multiply_first(step):
+            sim_first[step] = similarities(step % TOKENS, step // TOKENS, "first", 2, 1)
+
         def multiply(step):
             token = step % TOKENS
             if in_second_sweep(step):
-                times = 1 if in_first_sweep(step) else 2
+                times = 1 if first_sweeps(step) else 2
                 sim_second[step] = similarities(token, step // TOKENS - 1, "second", 3, times)
-            if in_first_sweep(step):
-                sim_first[step] = similarities(token, step // TOKENS, "first", 2, 1)
+            if step != CATCH_UP + 1:
+                for first in first_sweeps(step)[:1]:
+                    multiply_first(first)
 
         def subtract_top(step):
             if not in_second_sweep(step):
@@ -167,12 +192,35 @@ def tile_mug_head_kernel(tc, text_feat, video_feat, text_mask, out):
                     op0=ALU.add, op1=ALU.max,
                 )
 
-        def finish_top(step):
-            if in_first_sweep(step) and step % TOKENS == TOKENS - 1:
-                group = step // TOKENS
+        def catch_up(step):
+            if step == CATCH_UP:
+                for number, first in enumerate(first_sweeps(step)):
+                    if number > 0:
+                        multiply_first(first)
+                        raise_top(first, number % 2)
+                for first in first_sweeps(step + 1):
+                    multiply_first(first)
+
+        def finish_top(step, part):
+            if not in_first_sweep(step) or step % TOKENS < TOKENS - 1:
+                return
+            group = step // TOKENS
+            strands = 2 if (group, 1) in running_top else 1
+            if part == 0:
+                frame_tops[group] = group_work.tile(
+                    [P, strands, QUAD, GROUP_VIDEOS], F32, tag="frame_tops", name="frame_tops"
+                )
+                for strand in range(strands):
+                    nc.vector.tensor_reduce(
+                        out=frame_tops[group][:, strand, :, :],
+                        in_=running_top[group, strand][:].rearrange("a (q v b) -> a q b v", q=QUAD, v=QUAD),
+                        axis=INNERMOST,
+                        op=ALU.max,
+                    )
+            else:
                 nc.vector.tensor_reduce(
                     out=top[:, group_videos(group)],
-                    in_=running_top[group, 0][:].rearrange("a (v b) -> a b v", v=FRAMES),
+                    in_=frame_tops[group][:].rearrange("a s q b -> a b (s q)"),
                     axis=INNERMOST,
                     op=ALU.max,
                 )
@@ -250,22 +298,25 @@ def tile_mug_head_kernel(tc, text_feat, video_feat, text_mask, out):
                 return
             token = step % TOKENS
             group = step // TOKENS - 1
-            shares = [weights[step][:]]
+            shares = [[weights[step][:, k * P : (k + 1) * P] for k in range(BLOCKS)]]
             if token == TOKENS - QUAD + 1 and group in weight_sums:
-                shares.append(weight_sums[group][:].rearrange("a v b -> a (v b)"))
+                terms = weight_sums[group][:].rearrange("a v b -> a (v b)")
+                shares.append([terms[:, k * P : (k + 1) * P] for k in range(BLOCKS)])
+            if token == 0 and group == LAST:
+                shares.insert(0, [tiny_block[:] for k in range(BLOCKS)])
             if token == 0:
                 weight_banks[group] = psum.tile(
                     [P, BLOCKS, P], F32, tag="weight_sums", name="weight_sums", bufs=1
                 )
-            for terms in shares:
+            for number, blocks in enumerate(shares):
                 for k in range(BLOCKS):
                     transpose_add(
                         weight_banks[group][:, k, :],
-                        terms[:, k * P : (k + 1) * P],
-                        token == 0 and k == 0,
+                        blocks[k],
+                        token == 0 and number == 0 and k == 0,
                         token == TOKENS - 1 and k == BLOCKS - 1,
                     )
-            if token == TOKENS - 1:
+            if token == TOKENS - 1 and group != LAST:
                 store(group, 0, unit_blocks(TOKEN_UNIT), weight_banks[group][:])
 
         def unit_blocks(unit):
@@ -309,14 +360,19 @@ def tile_mug_head_kernel(tc, text_feat, video_feat, text_mask, out):
             multiply(step + 1)
             store_frame_sums(step - FRAME_LAG - 1)
             subtract_top(step)
-            raise_top(step)
+            for first in first_sweeps(step)[:1]:
+                raise_top(first)
             weigh(step)
-            form_product(step - 1)
-            finish_top(step)
-            add_up_products(step - 1)
-            add_up_gpsimd_weights(step - 1)
             add_up_weights(step - TOKEN_LAG)
             add_up_frames(step - FRAME_LAG)
+            catch_up(step)
+            for first in first_sweeps(step):
+                finish_top(first, 0)
+            form_product(step - 1)
+            for first in first_sweeps(step):
+                finish_top(first, 1)
+            add_up_products(step - 1)
+            add_up_gpsimd_weights(step - 1)
 
         first_text = FRAMES // QUAD
         batches = first_text + QUADS
@@ -341,7 +397,11 @@ def tile_mug_head_kernel(tc, text_feat, video_feat, text_mask, out):
                 else:
                     first = (batch - first_text) * QUAD
                     source = text_feat[:, first : first + QUAD, :]
-                nc.sync.dma_start(out=rows_of[batch][:], in_=source)
+                cuts = [0, QUAD // 2, QUAD] if batch == 0 else [0, QUAD]
+                for start, stop in zip(cuts, cuts[1:]):
+                    nc.sync.dma_start(
+                        out=rows_of[batch][:, start:stop, :], in_=source[:, start:stop, :]
+                    )
 
             def squares_on_vector(batch):
                 return [] if batch >= first_text + BLOCKS - 1 else [1, 3]
@@ -426,9 +486,6 @@ def tile_mug_head_kernel(tc, text_feat, video_feat, text_mask, out):
                 swept = slot - 3
                 if 0 <= slot - 2 < batches:
                     turn(slot - 2)
-                if swept == first_text - 1:
-                    for group in range(GROUPS):
-                        quantise_videos(group)
                 tokens = []
                 if first_text <= swept < batches:
                     quantise_texts(swept)
@@ -444,7 +501,6 @@ def tile_mug_head_kernel(tc, text_feat, video_feat, text_mask, out):
                 normalised = 0 <= slot - 1 < batches
                 if normalised:
                     norms = squares_of[slot - 1]
-                    nc.scalar.sqrt(out=norms[:], in_=norms[:])
                     nc.vector.tensor_scalar_max(out=norms[:], in0=norms[:], scalar1=EPS)
                 for filler in fillers[:1]:
                     filler()
@@ -454,32 +510,35 @@ def tile_mug_head_kernel(tc, text_feat, video_feat, text_mask, out):
                     filler()
                 if normalised:
                     normalise(slot - 1)
+                if swept == first_text - 1:
+                    for group in range(GROUPS):
+                        quantise_videos(group)
                 if slot < batches:
                     for i in range(QUAD):
                         if i not in squares_on_vector(slot):
                             add_up_squares(slot, i)
+                    nc.scalar.sqrt(out=squares_of[slot][:], in_=squares_of[slot][:])
                 if 0 <= slot - 2 < batches:
                     take_out(slot - 2)
                 for token in tokens[:2]:
                     raise_top(token, token % 2)
                 left_over = tokens[2:]
-            nc.vector.tensor_tensor(
-                out=running_top[0, 0][:], in0=running_top[0, 0][:], in1=running_top[0, 1][:], op=ALU.max
-            )
             multiply(TOKENS)
-            finish_top(TOKENS - 1)
+            for part in range(2):
+                finish_top(TOKENS - 1, part)
 
         quad_work = pools.enter_context(tc.tile_pool(name="quad_work", bufs=3))
         token_work = pools.enter_context(tc.tile_pool(name="token_work", bufs=4))
         finish = pools.enter_context(tc.tile_pool(name="finish", bufs=4))
-
-        last = GROUPS - 1
 
         def plain(work):
             return (False, work)
 
         def turning(work):
             return (True, work)
+
+        def reading(work):
+            return (None, work)
 
         result = finish.tile([P, P], F32, name="result", bufs=1)
 
@@ -502,12 +561,17 @@ def tile_mug_head_kernel(tc, text_feat, video_feat, text_mask, out):
 
             return [plain(repeat), turning(turn)]
 
+        def turn_products(group, tag, bufs):
+            bank = psum.tile([P, BLOCKS, P], F32, tag=tag, name="turned_products", bufs=bufs)
+            columns = product_sums[group][:].rearrange("a v b -> a (v b)")
+            for k in range(BLOCKS):
+                nc.tensor.transpose(bank[:, k, :], columns[:, k * P : (k + 1) * P], ident_f32[:])
+            return bank
+
         def turn_product_pieces(group):
+
             def turn(tag, bufs):
-                bank = psum.tile([P, BLOCKS, P], F32, tag=tag, name="turned_products", bufs=bufs)
-                columns = product_sums[group][:].rearrange("a v b -> a (v b)")
-                for k in range(BLOCKS):
-                    nc.tensor.transpose(bank[:, k, :], columns[:, k * P : (k + 1) * P], ident_f32[:])
+                bank = turn_products(group, tag, bufs)
                 return lambda: store(group, 1, unit_blocks(TOKEN_UNIT), bank[:])
 
             return [turning(turn)]
@@ -521,9 +585,11 @@ def tile_mug_head_kernel(tc, text_feat, video_feat, text_mask, out):
             weights = sums[:, group, 0, blocks, :]
             nc.scalar.activation(out=weights, in_=weights, func=FN.Exp, scale=-1.0)
 
-        def invert_block(group, block):
-            weights = sums[:, group, 0, block, :]
-            nc.vector.reciprocal(out=weights, in_=weights)
+        def invert_block(block):
+            weights = sums[:, LAST, 0, block, :]
+            over_tokens = block - TOKEN_UNIT * BLOCKS
+            source = weights if over_tokens < 0 else weight_banks[LAST][:, over_tokens, :]
+            nc.vector.reciprocal(out=weights, in_=source)
 
         def weighing_pieces(group, blocks, multiply_engine):
             weights = sums[:, group, 0, blocks, :]
@@ -547,21 +613,23 @@ def tile_mug_head_kernel(tc, text_feat, video_feat, text_mask, out):
 
             return [plain(divide), plain(deviate), plain(weigh_means), plain(form_products)]
 
-        def adding_pieces(group, unit):
+        def adding_pieces(group, units):
+            blocks = [block for unit in units for block in range(UNITS * BLOCKS)[unit_blocks(unit)]]
+
             def turn_back(tag, bufs):
                 bank = psum.tile(
                     [P, 2, QUAD, GROUP_VIDEOS], F32, tag=tag, name="turned_back", bufs=bufs
                 )
                 for plane in range(2):
-                    for k in range(BLOCKS):
+                    for block in blocks:
                         transpose_add(
                             bank[:, plane, :, :].rearrange("a s b -> a (s b)"),
-                            sums[:, group, plane, unit * BLOCKS + k, :],
-                            k == 0,
-                            k == BLOCKS - 1,
+                            sums[:, group, plane, block, :],
+                            block == blocks[0],
+                            block == blocks[-1],
                         )
                 return lambda: nc.vector.tensor_reduce(
-                    out=statistics[:, unit, :, group_videos(group)],
+                    out=statistics[:, units[0], :, group_videos(group)],
                     in_=bank[:].rearrange("a q s b -> a q b s"),
                     axis=INNERMOST,
                     op=ALU.add,
@@ -569,40 +637,52 @@ def tile_mug_head_kernel(tc, text_feat, video_feat, text_mask, out):
 
             return [turning(turn_back)]
 
-        def result_pieces(group):
-            videos = group_videos(group)
+        def result_pieces(groups, halves):
+            videos = slice(groups[0] * GROUP_VIDEOS, (groups[-1] + 1) * GROUP_VIDEOS)
+
+            def invert(unit):
+                weights = statistics[:, unit, 0, videos]
+                nc.vector.reciprocal(out=weights, in_=weights)
+
+            def divide(unit):
+                products = statistics[:, unit, 1, videos]
+                nc.vector.tensor_tensor(
+                    out=products, in0=products, in1=statistics[:, unit, 0, videos], op=ALU.mult
+                )
+
+            def add_mean(unit):
+                nc.vector.scalar_tensor_tensor(
+                    out=result[:, videos], in0=statistics[:, unit, 1, videos],
+                    scalar=half_mask_top[:, 0:1], in1=result[:, videos], op0=ALU.mult, op1=ALU.add,
+                )
 
             def join_halves():
-                halves = statistics[:, 0, :, videos]
+                joined = statistics[:, 0, :, videos]
                 nc.vector.tensor_tensor(
-                    out=halves, in0=halves, in1=statistics[:, 1, :, videos], op=ALU.add
+                    out=joined, in0=joined, in1=statistics[:, 1, :, videos], op=ALU.add
                 )
 
-            def divide():
-                for unit in (0, TOKEN_UNIT):
-                    weights = statistics[:, unit, 0, videos]
-                    nc.vector.reciprocal(out=weights, in_=weights)
-                for unit in (0, TOKEN_UNIT):
-                    products = statistics[:, unit, 1, videos]
-                    nc.vector.tensor_tensor(
-                        out=products, in0=products, in1=statistics[:, unit, 0, videos], op=ALU.mult
-                    )
+            def invert_both():
+                invert(TOKEN_UNIT)
+                invert(0)
+
+            def divide_both():
+                divide(TOKEN_UNIT)
+                divide(0)
+                add_mean(TOKEN_UNIT)
 
             def put_out():
-                nc.vector.tensor_tensor(
-                    out=result[:, videos], in0=statistics[:, 0, 1, videos],
-                    in1=statistics[:, TOKEN_UNIT, 1, videos], op=ALU.add,
-                )
-                nc.vector.scalar_tensor_tensor(
-                    out=result[:, videos], in0=result[:, videos], scalar=0.5, in1=top[:, videos],
-                    op0=ALU.mult, op1=ALU.add,
-                )
-                nc.vector.tensor_scalar_mul(
-                    out=result[:, videos], in0=result[:, videos], scalar1=mask_top[:, 0:1]
-                )
+                add_mean(0)
                 nc.sync.dma_start(out=out[:, videos], in_=result[:, videos])
 
-            return [plain(join_halves), plain(divide), plain(put_out)]
+            joining = [reading(join_halves)] if halves else []
+            return joining + [reading(invert_both), plain(divide_both), plain(put_out)]
+
+        def scale_top_pieces(group):
+            videos = group_videos(group)
+            return [plain(lambda: nc.vector.tensor_scalar_mul(
+                out=result[:, videos], in0=top[:, videos], scalar1=mask_top[:, 0:1]
+            ))]
 
         def woven(chains):
             pieces = []
@@ -620,48 +700,80 @@ def tile_mug_head_kernel(tc, text_feat, video_feat, text_mask, out):
         def group_chains(groups):
             chains = []
             for group in groups:
+                adding = ([], adding_pieces(group, range(TOKEN_UNIT)), adding_pieces(group, [TOKEN_UNIT]))
                 for unit in range(UNITS):
                     blocks = unit_blocks(unit)
                     invert = plain(lambda group=group, blocks=blocks: invert_logarithms(group, blocks))
                     weighing = weighing_pieces(group, blocks, nc.gpsimd)
-                    chains.append([invert] + weighing + adding_pieces(group, unit))
+                    chains.append([invert] + weighing + adding[unit])
             return chains
 
-        for number, groups in enumerate((list(range(last - 1)), [last - 1])):
+        for number, groups in enumerate((list(range(LAST - 1)), [LAST - 1])):
             swept = (groups[-1] + 2) * TOKENS
             stored = swept + FRAME_LAG
-            wait_for(number, swept, woven([turn_top_pieces(group) for group in groups]))
+            wait_for(number, swept, woven([
+                turn_top_pieces(group) + scale_top_pieces(group) for group in groups
+            ]))
             wait_for(number, swept, woven([turn_product_pieces(group) for group in groups]))
-            wait_for(number, stored, [plain(lambda groups=groups: take_logarithms(groups))])
+            logarithms = max(stored, LOG_STEP)
+            wait_for(number, logarithms, [plain(lambda groups=groups: take_logarithms(groups))])
             wait_for(number, stored, woven(group_chains(groups)))
-            for group in groups:
-                wait_for(number, stored, result_pieces(group))
+            wait_for(number, stored, result_pieces(groups, False))
 
         def quad_stored(quad):
             return FIRST_STEPS + (quad + 1) * QUAD + FRAME_LAG
 
-        def inversions(blocks):
-            return [plain(lambda block=block: invert_block(last, block)) for block in blocks]
-
-        wait_for(2, FIRST_STEPS, turn_top_pieces(last))
+        wait_for(2, FIRST_STEPS, turn_top_pieces(LAST) + scale_top_pieces(LAST))
         for quad in range(QUADS - 1):
-            wait_for(2, quad_stored(quad), inversions([quad]))
+            wait_for(2, quad_stored(quad), [plain(lambda quad=quad: invert_block(quad))])
             if quad == BLOCKS - 1:
-                wait_for(2, quad_stored(quad), weighing_pieces(last, unit_blocks(0), nc.gpsimd))
-                wait_for(2, quad_stored(quad), adding_pieces(last, 0))
-        early = weighing_pieces(last, slice(BLOCKS, QUADS - 1), nc.gpsimd)
-        columns = unit_blocks(TOKEN_UNIT)
-        wait_for(2, quad_stored(QUADS - 2), early[:2])
-        wait_for(2, STEPS + 1, inversions(range(QUADS, QUADS + 2)))
-        wait_for(2, STEPS + 1, early[2:])
-        wait_for(2, STEPS + FRAME_LAG - 1, turn_product_pieces(last))
-        wait_for(2, STEPS + FRAME_LAG - 1, inversions([QUADS - 1]))
-        wait_for(2, STEPS + FRAME_LAG, inversions(range(QUADS + 2, UNITS * BLOCKS)))
-        wait_for(2, STEPS + FRAME_LAG, woven([
-            weighing_pieces(last, slice(QUADS - 1, QUADS), nc.vector) + adding_pieces(last, 1),
-            weighing_pieces(last, columns, nc.vector) + adding_pieces(last, TOKEN_UNIT),
-        ]))
-        wait_for(2, STEPS + FRAME_LAG, result_pieces(last))
+                wait_for(2, quad_stored(quad), weighing_pieces(LAST, unit_blocks(0), nc.gpsimd))
+                wait_for(2, quad_stored(quad), adding_pieces(LAST, [0]))
+        wait_for(
+            2, quad_stored(QUADS - 2), weighing_pieces(LAST, slice(BLOCKS, QUADS - 1), nc.gpsimd)
+        )
+
+        def finish_last_group(turned_products):
+            first_block = TOKEN_UNIT * BLOCKS
+
+            def works(blocks):
+                return [work for turns, work in weighing_pieces(LAST, blocks, nc.vector)]
+
+            def divide(first, stop):
+                blocks = slice(first_block + first, first_block + stop)
+                nc.vector.scalar_tensor_tensor(
+                    out=sums[:, LAST, 1, blocks, :], in0=turned_products[:, first:stop, :],
+                    scalar=nudge[:, 1:2], in1=sums[:, LAST, 0, blocks, :], op0=ALU.add, op1=ALU.mult,
+                )
+
+            deviate_a, weigh_a, form_a = works(slice(first_block, first_block + 2))[1:]
+            deviate_b, weigh_b, form_b = works(slice(first_block + 2, first_block + BLOCKS))[1:]
+            divide_quad, deviate_quad, weigh_quad, form_quad = works(slice(QUADS - 1, QUADS))
+            for block in range(first_block, first_block + 3):
+                invert_block(block)
+            divide(0, 2)
+            invert_block(first_block + 3)
+            deviate_a()
+            weigh_a()
+            divide(2, BLOCKS)
+            invert_block(QUADS - 1)
+            deviate_b()
+            weigh_b()
+            form_a()
+            divide_quad()
+            form_b()
+            deviate_quad()
+            weigh_quad()
+            form_quad()
+            added = [
+                work("first", 2)
+                for unit in (TOKEN_UNIT, 1)
+                for turns, work in adding_pieces(LAST, [unit])
+            ]
+            for reader in added:
+                reader()
+            for turns, work in result_pieces([LAST], True):
+                work()
 
         readers = []
 
@@ -682,6 +794,8 @@ def tile_mug_head_kernel(tc, text_feat, video_feat, text_mask, out):
             for step in range(TOKENS, STEPS + FRAME_LAG + 1):
                 pipeline_step(step)
                 read_turned()
+                if step == STEPS + TOKEN_LAG - 1:
+                    turned_products = turn_products(LAST, "first", 2)
                 sweeping = step < FIRST_STEPS
                 tag = "quad_sums%d" % (1 - (step - FRAME_LAG) % QUAD // 2) if sweeping else "first"
                 for number, most in enumerate((PIECES_PER_STEP, PIECES_PER_STEP, 1)):
@@ -690,13 +804,16 @@ def tile_mug_head_kernel(tc, text_feat, video_feat, text_mask, out):
                         if not queue or queue[0][0] > step:
                             break
                         turns = queue[0][1][0]
+                        if turns is None and readers:
+                            break
                         if turns and (readers if sweeping or number < 2 else len(readers) > 1):
                             break
                         if turns and sweeping and step % 2 == 1:
                             break
                         serve(queue, tag, 1 if sweeping else 2)
+            read_turned()
             for queue in queues:
                 while queue:
                     serve(queue, "first", 2)
-                    if len(readers) > 1 or not queue or not queue[0][1][0]:
-                        read_turned()
+                    read_turned()
+            finish_last_group(turned_products)

@@ -90,7 +90,13 @@ def tile_mug_head_kernel(tc, text_feat, video_feat, text_mask, out):
         video_scales = keep.tile([P, GROUPS * GROUP_COLS], U8, name="video_scales", align_bytes=64)
         top = keep.tile([P, P], F32, name="top")
         top_turned = keep.tile([P, GROUPS, P], F32, name="top_turned")
-        sums = keep.tile([P, GROUPS, 2, UNITS * BLOCKS, P], F32, name="sums")
+        sums = {
+            (group, plane): keep.tile(
+                [P, UNITS * BLOCKS, P], F32, tag="sums_%d_%d" % (group, plane), name="sums"
+            )
+            for group in range(GROUPS)
+            for plane in range(2)
+        }
         statistics = keep.tile([P, UNITS, 2, P], F32, name="statistics")
 
         def transpose_add(acc, block, start, stop):
@@ -324,7 +330,7 @@ def tile_mug_head_kernel(tc, text_feat, video_feat, text_mask, out):
 
         def store(group, plane, blocks, source):
             nc.scalar.activation(
-                out=sums[:, group, plane, blocks, :], in_=source, func=FN.Identity,
+                out=sums[group, plane][:, blocks, :], in_=source, func=FN.Identity,
                 bias=nudge[:, plane : plane + 1],
             )
 
@@ -578,22 +584,22 @@ def tile_mug_head_kernel(tc, text_feat, video_feat, text_mask, out):
 
         def take_logarithms(groups):
             for group in groups:
-                weights = sums[:, group, 0, :, :]
+                weights = sums[group, 0][:, :, :]
                 nc.scalar.activation(out=weights, in_=weights, func=FN.Ln)
 
         def invert_logarithms(group, blocks):
-            weights = sums[:, group, 0, blocks, :]
+            weights = sums[group, 0][:, blocks, :]
             nc.scalar.activation(out=weights, in_=weights, func=FN.Exp, scale=-1.0)
 
         def invert_block(block):
-            weights = sums[:, LAST, 0, block, :]
+            weights = sums[LAST, 0][:, block, :]
             over_tokens = block - TOKEN_UNIT * BLOCKS
             source = weights if over_tokens < 0 else weight_banks[LAST][:, over_tokens, :]
             nc.vector.reciprocal(out=weights, in_=source)
 
         def weighing_pieces(group, blocks, multiply_engine):
-            weights = sums[:, group, 0, blocks, :]
-            means = sums[:, group, 1, blocks, :]
+            weights = sums[group, 0][:, blocks, :]
+            means = sums[group, 1][:, blocks, :]
 
             def divide():
                 multiply_engine.tensor_tensor(out=means, in0=means, in1=weights, op=ALU.mult)
@@ -624,7 +630,7 @@ def tile_mug_head_kernel(tc, text_feat, video_feat, text_mask, out):
                     for block in blocks:
                         transpose_add(
                             bank[:, plane, :, :].rearrange("a s b -> a (s b)"),
-                            sums[:, group, plane, block, :],
+                            sums[group, plane][:, block, :],
                             block == blocks[0],
                             block == blocks[-1],
                         )
@@ -742,15 +748,13 @@ def tile_mug_head_kernel(tc, text_feat, video_feat, text_mask, out):
             def divide(first, stop):
                 blocks = slice(first_block + first, first_block + stop)
                 nc.vector.scalar_tensor_tensor(
-                    out=sums[:, LAST, 1, blocks, :], in0=turned_products[:, first:stop, :],
-                    scalar=nudge[:, 1:2], in1=sums[:, LAST, 0, blocks, :], op0=ALU.add, op1=ALU.mult,
+                    out=sums[LAST, 1][:, blocks, :], in0=turned_products[:, first:stop, :],
+                    scalar=nudge[:, 1:2], in1=sums[LAST, 0][:, blocks, :], op0=ALU.add, op1=ALU.mult,
                 )
 
             deviate_a, weigh_a, form_a = works(slice(first_block, first_block + 2))[1:]
             deviate_b, weigh_b, form_b = works(slice(first_block + 2, first_block + BLOCKS))[1:]
             divide_quad, deviate_quad, weigh_quad, form_quad = works(slice(QUADS - 1, QUADS))
-            for block in range(first_block, first_block + 3):
-                invert_block(block)
             divide(0, 2)
             invert_block(first_block + 3)
             deviate_a()
@@ -796,6 +800,8 @@ def tile_mug_head_kernel(tc, text_feat, video_feat, text_mask, out):
                 read_turned()
                 if step == STEPS + TOKEN_LAG - 1:
                     turned_products = turn_products(LAST, "first", 2)
+                    for block in range(TOKEN_UNIT * BLOCKS, UNITS * BLOCKS - 1):
+                        invert_block(block)
                 sweeping = step < FIRST_STEPS
                 tag = "quad_sums%d" % (1 - (step - FRAME_LAG) % QUAD // 2) if sweeping else "first"
                 for number, most in enumerate((PIECES_PER_STEP, PIECES_PER_STEP, 1)):

from contextlib import ExitStack

import concourse.mybir as mybir
from concourse.masks import make_identity

F32 = mybir.dt.float32
BF16 = mybir.dt.bfloat16
U32 = mybir.dt.uint32
U8 = mybir.dt.uint8
FP8X4 = mybir.dt.float8_e4m3fn_x4
ALU = mybir.AluOpType
FN = mybir.ActivationFunctionType
INNERMOST = mybir.AxisListType.X

P = 128
TOKENS = 32
FRAMES = 16
FEATURES = 512
PACK = 4
TAU = 100.0
EPS = 1.0e-6
BARRED = -1.0e30
TINY = 1.0e-30
LOW = -1.0e-20

GROUPS = 4
LAST = GROUPS - 1
GROUP_VIDEOS = P // GROUPS
GROUP_COLS = FRAMES * GROUP_VIDEOS
BLOCKS = GROUP_COLS // P
QUAD = 4
QUADS = TOKENS // QUAD
UNITS = QUADS // BLOCKS + 1
TOKEN_UNIT = UNITS - 1

FIRST_STEPS = GROUPS * TOKENS
STEPS = FIRST_STEPS + TOKENS
SECOND_LEVEL = FIRST_STEPS - TOKENS
LOG_STEP = SECOND_LEVEL + 7
CATCH_UP = LOG_STEP + 2
AHEAD = 6
FRAME_LAG = 4
TOKEN_LAG = 2
PIECES_PER_STEP = 2

FLOPS = 2 * (P * TOKENS) * (P * FRAMES) * FEATURES


def tile_mug_head_kernel(tc, text_feat, video_feat, text_mask, out):
    nc = tc.nc
    with ExitStack() as pools:
        consts = pools.enter_context(tc.tile_pool(name="consts", bufs=1))
        keep = pools.enter_context(tc.tile_pool(name="keep", bufs=1))
        psum = pools.enter_context(tc.psum_pool(name="psum", bufs=2))

        ident_f32 = consts.tile([P, P], F32, name="ident_f32")
        make_identity(nc, ident_f32[:])

        mask_bf16 = consts.tile([P, TOKENS], BF16, name="mask_bf16")
        nc.sync.dma_start(out=mask_bf16[:], in_=text_mask)
        mask = consts.tile([P, TOKENS], F32, name="mask")
        nc.vector.tensor_copy(out=mask[:], in_=mask_bf16[:])
        sharp_mask = consts.tile([P, TOKENS], F32, name="sharp_mask")
        nc.vector.tensor_scalar_mul(out=sharp_mask[:], in0=mask[:], scalar1=TAU)
        barred = consts.tile([P, TOKENS], F32, name="barred")
        nc.vector.tensor_scalar(
            out=barred[:], in0=mask[:], scalar1=0.0, scalar2=BARRED, op0=ALU.is_equal, op1=ALU.mult
        )
        mask_top = consts.tile([P, 1], F32, name="mask_top")
        nc.vector.tensor_reduce(out=mask_top[:], in_=mask[:], axis=INNERMOST, op=ALU.max)
        sharp_top = consts.tile([P, 1], F32, name="sharp_top")
        nc.vector.tensor_scalar_mul(out=sharp_top[:], in0=mask_top[:], scalar1=TAU)
        half_mask_top = consts.tile([P, 1], F32, name="half_mask_top")
        nc.vector.tensor_scalar_mul(out=half_mask_top[:], in0=mask_top[:], scalar1=0.5)
        nudge = consts.tile([P, 2], F32, name="nudge")
        for plane, value in enumerate((TINY, LOW)):
            nc.vector.tensor_scalar(
                out=nudge[:, plane : plane + 1], in0=mask_top[:], scalar1=0.0, scalar2=value,
                op0=ALU.mult, op1=ALU.add,
            )

        tiny_block = consts.tile([P, P], F32, name="tiny_block")
        nc.vector.tensor_scalar(
            out=tiny_block[:], in0=ident_f32[:], scalar1=0.0, scalar2=TINY, op0=ALU.mult, op1=ALU.add
        )

        text_codes = keep.tile([P, TOKENS * P], U32, name="text_codes", align_bytes=64)
        text_scales = keep.tile([P, TOKENS * P], U8, name="text_scales", align_bytes=64)
        video_codes = keep.tile([P, GROUPS * GROUP_COLS], U32, name="video_codes", align_bytes=64)
        video_scales = keep.tile([P, GROUPS * GROUP_COLS], U8, name="video_scales", align_bytes=64)
        top = keep.tile([P, P], F32, name="top")
        top_turned = keep.tile([P, GROUPS, P], F32, name="top_turned")
        sums = {
            (group, plane): keep.tile(
                [P, UNITS * BLOCKS, P], F32, tag="sums_%d_%d" % (group, plane), name="sums"
            )
            for group in range(GROUPS)
            for plane in range(2)
        }
        statistics = keep.tile([P, UNITS, 2, P], F32, name="statistics")

        def transpose_add(acc, block, start, stop):
            nc.tensor.matmul(
                out=acc, lhsT=block, rhs=ident_f32[:], is_transpose=True, start=start, stop=stop
            )

        group_work = pools.enter_context(tc.tile_pool(name="group_work", bufs=GROUPS))

        def similarities(token, group, tag, bufs, times):
            sim = psum.tile([P, GROUP_COLS], F32, tag=tag, name="sim", bufs=bufs)
            texts = slice(token * P, (token + 1) * P)
            cols = slice(group * GROUP_COLS, (group + 1) * GROUP_COLS)
            for repeat in range(times):
                nc.tensor.matmul_mx(
                    out=sim[:],
                    lhsT=text_codes[:, texts].bitcast(FP8X4),
                    lhsT_scale=text_scales[:, texts],
                    rhs=video_codes[:, cols].bitcast(FP8X4),
                    rhs_scale=video_scales[:, cols],
                    start=True,
                    stop=True,
                )
            return sim

        sim_first = {}
        sim_second = {}
        running_top = {}
        frame_tops = {}
        deviations = {}
        weights = {}
        weight_sums = {}
        quad_tiles = {}
        product_sums = {}
        quad_banks = {}
        weight_banks = {}

        def in_first_sweep(step):
            return 0 <= step < FIRST_STEPS

        def first_sweeps(step):
            if step < CATCH_UP:
                steps = [step]
            elif step == CATCH_UP:
                steps = list(range(step, step + AHEAD + 1))
            else:
                steps = [step + AHEAD]
            return [first for first in steps if in_first_sweep(first)]

        def in_second_sweep(step):
            return TOKENS <= step < STEPS

        def weighed_by_gpsimd(step):
            return step < SECOND_LEVEL and step % QUAD == 1 and step % TOKENS < TOKENS - QUAD

        def group_videos(group):
            return slice(group * GROUP_VIDEOS, (group + 1) * GROUP_VIDEOS)

        def multiply_first(step):
            sim_first[step] = similarities(step % TOKENS, step // TOKENS, "first", 2, 1)

        def multiply(step):
            token = step % TOKENS
            if in_second_sweep(step):
                times = 1 if first_sweeps(step) else 2
                sim_second[step] = similarities(token, step // TOKENS - 1, "second", 3, times)
            if step != CATCH_UP + 1:
                for first in first_sweeps(step)[:1]:
                    multiply_first(first)

        def subtract_top(step):
            if not in_second_sweep(step):
                return
            group = step // TOKENS - 1
            deviations[step] = token_work.tile([P, GROUP_COLS], F32, tag="deviation", name="deviation")
            nc.vector.tensor_tensor(
                out=deviations[step][:].rearrange("a (v b) -> a v b", v=FRAMES),
                in0=sim_second[step][:].rearrange("a (v b) -> a v b", v=FRAMES),
                in1=top[:, group_videos(group)].unsqueeze(1).to_broadcast([P, FRAMES, GROUP_VIDEOS]),
                op=ALU.subtract,
            )

        def raise_top(step, strand=0):
            if not in_first_sweep(step):
                return
            token = step % TOKENS
            group = step // TOKENS
            bar = barred[:, token : token + 1]
            if (group, strand) not in running_top:
                running = group_work.tile([P, GROUP_COLS], F32, tag="running", name="running")
                running_top[group, strand] = running
                nc.vector.tensor_scalar(
                    out=running[:], in0=sim_first[step][:], scalar1=bar, scalar2=None, op0=ALU.add
                )
            else:
                running = running_top[group, strand]
                nc.vector.scalar_tensor_tensor(
                    out=running[:], in0=sim_first[step][:], scalar=bar, in1=running[:],
                    op0=ALU.add, op1=ALU.max,
                )

        def catch_up(step):
            if step == CATCH_UP:
                for number, first in enumerate(first_sweeps(step)):
                    if number > 0:
                        multiply_first(first)
                        raise_top(first, number % 2)
                for first in first_sweeps(step + 1):
                    multiply_first(first)

        def finish_top(step, part):
            if not in_first_sweep(step) or step % TOKENS < TOKENS - 1:
                return
            group = step // TOKENS
            strands = 2 if (group, 1) in running_top else 1
            if part == 0:
                frame_tops[group] = group_work.tile(
                    [P, strands, QUAD, GROUP_VIDEOS], F32, tag="frame_tops", name="frame_tops"
                )
                for strand in range(strands):
                    nc.vector.tensor_reduce(
                        out=frame_tops[group][:, strand, :, :],
                        in_=running_top[group, strand][:].rearrange("a (q v b) -> a q b v", q=QUAD, v=QUAD),
                        axis=INNERMOST,
                        op=ALU.max,
                    )
            else:
                nc.vector.tensor_reduce(
                    out=top[:, group_videos(group)],
                    in_=frame_tops[group][:].rearrange("a s q b -> a b (s q)"),
                    axis=INNERMOST,
                    op=ALU.max,
                )

        def weigh(step):
            if not in_second_sweep(step):
                return
            token = step % TOKENS
            if step % QUAD == 0:
                quad_shape = [P, FRAMES, QUAD, GROUP_VIDEOS]
                quad_tiles[step // QUAD] = (
                    quad_work.tile(quad_shape, F32, tag="quad_weights", name="quad_weights"),
                    quad_work.tile(quad_shape, F32, tag="quad_products", name="quad_products"),
                )
            targets = [
                (
                    quad_tiles[step // QUAD][0][:, :, step % QUAD, :],
                    deviations[step][:].rearrange("a (v b) -> a v b", v=FRAMES),
                )
            ]
            if not weighed_by_gpsimd(step):
                weights[step] = token_work.tile([P, GROUP_COLS], F32, tag="weight", name="weight")
                targets.append((weights[step][:], deviations[step][:]))
            for target, source in targets:
                nc.scalar.activation(
                    out=target, in_=source, func=FN.Exp,
                    scale=sharp_mask[:, token : token + 1], bias=barred[:, token : token + 1],
                )

        def form_product(step):
            if not in_second_sweep(step):
                return
            nc.vector.tensor_tensor(
                out=quad_tiles[step // QUAD][1][:, :, step % QUAD, :],
                in0=sim_second[step][:].rearrange("a (v b) -> a v b", v=FRAMES),
                in1=quad_tiles[step // QUAD][0][:, :, step % QUAD, :],
                op=ALU.mult,
            )

        def add_up_products(step):
            if not in_second_sweep(step):
                return
            group = step // TOKENS - 1
            products = quad_tiles[step // QUAD][1]
            if step % TOKENS == 0:
                product_sums[group] = group_work.tile(
                    [P, FRAMES, GROUP_VIDEOS], F32, tag="product_sums", name="product_sums"
                )
                return
            acc = product_sums[group]
            so_far = products[:, :, 0, :] if step % TOKENS == 1 else acc[:]
            nc.gpsimd.tensor_tensor(
                out=acc[:], in0=so_far, in1=products[:, :, step % QUAD, :], op=ALU.add
            )

        def add_up_gpsimd_weights(step):
            if not in_second_sweep(step) or not weighed_by_gpsimd(step):
                return
            group = step // TOKENS - 1
            terms = quad_tiles[step // QUAD][0][:, :, step % QUAD, :]
            if step % TOKENS == 1:
                weight_sums[group] = group_work.tile(
                    [P, FRAMES, GROUP_VIDEOS], F32, tag="weight_sums", name="weight_sums"
                )
                nc.gpsimd.tensor_scalar(
                    out=weight_sums[group][:], in0=terms, scalar1=1.0, scalar2=0.0,
                    op0=ALU.mult, op1=ALU.add,
                )
            else:
                acc = weight_sums[group]
                nc.gpsimd.tensor_tensor(out=acc[:], in0=acc[:], in1=terms, op=ALU.add)

        def add_up_weights(step):
            if not in_second_sweep(step) or weighed_by_gpsimd(step):
                return
            token = step % TOKENS
            group = step // TOKENS - 1
            shares = [[weights[step][:, k * P : (k + 1) * P] for k in range(BLOCKS)]]
            if token == TOKENS - QUAD + 1 and group in weight_sums:
                terms = weight_sums[group][:].rearrange("a v b -> a (v b)")
                shares.append([terms[:, k * P : (k + 1) * P] for k in range(BLOCKS)])
            if token == 0 and group == LAST:
                shares.insert(0, [tiny_block[:] for k in range(BLOCKS)])
            if token == 0:
                weight_banks[group] = psum.tile(
                    [P, BLOCKS, P], F32, tag="weight_sums", name="weight_sums", bufs=1
                )
            for number, blocks in enumerate(shares):
                for k in range(BLOCKS):
                    transpose_add(
                        weight_banks[group][:, k, :],
                        blocks[k],
                        token == 0 and number == 0 and k == 0,
                        token == TOKENS - 1 and k == BLOCKS - 1,
                    )
            if token == TOKENS - 1 and group != LAST:
                store(group, 0, unit_blocks(TOKEN_UNIT), weight_banks[group][:])

        def unit_blocks(unit):
            return slice(unit * BLOCKS, (unit + 1) * BLOCKS)

        def store(group, plane, blocks, source):
            nc.scalar.activation(
                out=sums[group, plane][:, blocks, :], in_=source, func=FN.Identity,
                bias=nudge[:, plane : plane + 1],
            )

        def add_up_frames(step):
            if not in_second_sweep(step):
                return
            quad = step // QUAD
            plane = (step % QUAD) // 2
            first_frame = (step % 2) * (FRAMES // 2)
            if step % 2 == 0:
                quad_banks[quad, plane] = psum.tile(
                    [P, 1, P], F32, tag="quad_sums%d" % plane, name="quad_sums", bufs=1
                )
            for v in range(first_frame, first_frame + FRAMES // 2):
                transpose_add(
                    quad_banks[quad, plane][:, 0, :],
                    quad_tiles[quad][plane][:, v, :, :].rearrange("a s b -> a (s b)"),
                    v == 0,
                    v == FRAMES - 1,
                )

        def store_frame_sums(step):
            if not in_second_sweep(step) or step % 2 == 0:
                return
            block = step % TOKENS // QUAD
            plane = (step % QUAD) // 2
            store(
                step // TOKENS - 1, plane, slice(block, block + 1),
                quad_banks[step // QUAD, plane][:],
            )

        def pipeline_step(step):
            multiply(step + 1)
            store_frame_sums(step - FRAME_LAG - 1)
            subtract_top(step)
            for first in first_sweeps(step)[:1]:
                raise_top(first)
            weigh(step)
            add_up_weights(step - TOKEN_LAG)
            add_up_frames(step - FRAME_LAG)
            catch_up(step)
            for first in first_sweeps(step):
                finish_top(first, 0)
            form_product(step - 1)
            for first in first_sweeps(step):
                finish_top(first, 1)
            add_up_products(step - 1)
            add_up_gpsimd_weights(step - 1)

        first_text = FRAMES // QUAD
        batches = first_text + QUADS
        rows_of = {}
        squares_of = {}
        normal_of = {}
        turned_of = {}
        grouped_of = {}

        with tc.manual_schedule(), tc.tile_pool(name="prep", bufs=3) as prep:
            warm = prep.tile([P, 1], F32, name="warm", bufs=1)
            nc.vector.memset(warm[:], 1.0)
            nc.scalar.sqrt(out=warm[:], in_=warm[:])
            video_grouped = prep.tile(
                [P, GROUPS * GROUP_COLS * PACK], BF16, name="video_grouped", bufs=1, align_bytes=64
            )

            def load(batch):
                rows_of[batch] = prep.tile([P, QUAD, FEATURES], BF16, tag="raw", name="raw", bufs=batches)
                if batch < first_text:
                    source = video_feat[:, batch * QUAD : (batch + 1) * QUAD, :]
                else:
                    first = (batch - first_text) * QUAD
                    source = text_feat[:, first : first + QUAD, :]
                cuts = [0, QUAD // 2, QUAD] if batch == 0 else [0, QUAD]
                for start, stop in zip(cuts, cuts[1:]):
                    nc.sync.dma_start(
                        out=rows_of[batch][:, start:stop, :], in_=source[:, start:stop, :]
                    )

            def squares_on_vector(batch):
                return [] if batch >= first_text + BLOCKS - 1 else [1, 3]

            def add_up_squares(batch, i):
                if batch not in squares_of:
                    squares_of[batch] = prep.tile([P, QUAD], F32, tag="squares", name="squares")
                row = rows_of[batch][:, i, :]
                total = squares_of[batch][:, i : i + 1]
                if i in squares_on_vector(batch):
                    scratch = prep.tile([P, FEATURES], BF16, tag="scratch_v", name="scratch_v")
                    nc.vector.scalar_tensor_tensor(
                        out=scratch[:], in0=row, scalar=1.0, in1=row,
                        op0=ALU.mult, op1=ALU.mult, accum_out=total,
                    )
                else:
                    scratch = prep.tile([P, FEATURES], BF16, tag="scratch_s", name="scratch_s")
                    nc.scalar.activation(out=scratch[:], in_=row, func=FN.Square, accum_out=total)

            def normalise(batch):
                normal = prep.tile([P, QUAD, FEATURES], BF16, tag="normal", name="normal")
                normal_of[batch] = normal
                for i in range(QUAD):
                    inverse = squares_of[batch][:, i : i + 1]
                    nc.vector.tensor_scalar_mul(
                        out=normal[:, i, :], in0=rows_of[batch][:, i, :], scalar1=inverse
                    )

            def turn(batch):
                for pair in range(0, QUAD, 2):
                    bank = psum.tile([P, 2, 2, P], F32, tag="second", name="turned_rows", bufs=3)
                    turned_of[batch, pair] = bank
                    for i in range(2):
                        words = normal_of[batch][:, pair + i, :].bitcast(F32)
                        for u in range(2):
                            nc.tensor.transpose(
                                bank[:, i, u, :], words[:, u : FEATURES // 2 : 2], ident_f32[:]
                            )

            def take_out(batch):
                if batch >= first_text:
                    grouped_of[batch] = prep.tile(
                        [P, QUAD * P * PACK], BF16, tag="text_grouped", name="text_grouped", align_bytes=64
                    )
                for pair in range(0, QUAD, 2):
                    bank = turned_of[batch, pair]
                    if batch >= first_text:
                        target = grouped_of[batch][:].bitcast(F32)
                        nc.scalar.copy(
                            out=target.rearrange("p (s a u) -> p s a u", s=QUAD, u=2)[:, pair : pair + 2],
                            in_=bank[:].rearrange("p s u a -> p s a u"),
                        )
                    else:
                        target = video_grouped[:].bitcast(F32)
                        target = target.rearrange("p (g v b u) -> p g v b u", g=GROUPS, v=FRAMES, u=2)
                        for i in range(2):
                            nc.scalar.copy(
                                out=target[:, :, batch * QUAD + pair + i],
                                in_=bank[:, i, :, :].rearrange("p u (g b) -> p g b u", g=GROUPS),
                            )

            def quantise_videos(group):
                cols = slice(group * GROUP_COLS, (group + 1) * GROUP_COLS)
                values = slice(group * GROUP_COLS * PACK, (group + 1) * GROUP_COLS * PACK)
                nc.vector.quantize_mx(
                    out=video_codes[:, cols].bitcast(FP8X4), scales=video_scales[:, cols],
                    in_=video_grouped[:, values],
                )

            def quantise_texts(batch):
                first = (batch - first_text) * QUAD * P
                cols = slice(first, first + QUAD * P)
                nc.vector.quantize_mx(
                    out=text_codes[:, cols].bitcast(FP8X4), scales=text_scales[:, cols],
                    in_=grouped_of[batch][:],
                )

            for batch in range(batches):
                load(batch)
            left_over = []
            for slot in range(batches + 4):
                swept = slot - 3
                if 0 <= slot - 2 < batches:
                    turn(slot - 2)
                tokens = []
                if first_text <= swept < batches:
                    quantise_texts(swept)
                    first = (swept - first_text) * QUAD
                    tokens = list(range(first, first + QUAD))
                for token, tag in zip(tokens, ("first", "first", "quad_sums0", "quad_sums1")):
                    sim_first[token] = similarities(token, 0, tag, 2 if tag == "first" else 1, 1)
                fillers = [lambda token=token: raise_top(token, token % 2) for token in left_over]
                if slot < batches:
                    fillers.extend([
                        lambda i=i, slot=slot: add_up_squares(slot, i) for i in squares_on_vector(slot)
                    ])
                normalised = 0 <= slot - 1 < batches
                if normalised:
                    norms = squares_of[slot - 1]
                    nc.vector.tensor_scalar_max(out=norms[:], in0=norms[:], scalar1=EPS)
                for filler in fillers[:1]:
                    filler()
                if normalised:
                    nc.vector.reciprocal(out=norms[:], in_=norms[:])
                for filler in fillers[1:]:
                    filler()
                if normalised:
                    normalise(slot - 1)
                if swept == first_text - 1:
                    for group in range(GROUPS):
                        quantise_videos(group)
                if slot < batches:
                    for i in range(QUAD):
                        if i not in squares_on_vector(slot):
                            add_up_squares(slot, i)
                    nc.scalar.sqrt(out=squares_of[slot][:], in_=squares_of[slot][:])
                if 0 <= slot - 2 < batches:
                    take_out(slot - 2)
                for token in tokens[:2]:
                    raise_top(token, token % 2)
                left_over = tokens[2:]
            multiply(TOKENS)
            for part in range(2):
                finish_top(TOKENS - 1, part)

        quad_work = pools.enter_context(tc.tile_pool(name="quad_work", bufs=3))
        token_work = pools.enter_context(tc.tile_pool(name="token_work", bufs=4))
        finish = pools.enter_context(tc.tile_pool(name="finish", bufs=4))

        def plain(work):
            return (False, work)

        def turning(work):
            return (True, work)

        def reading(work):
            return (None, work)

        result = finish.tile([P, P], F32, name="result", bufs=1)

        def turn_top_pieces(group):
            made = {}

            def repeat():
                made["repeated"] = finish.tile([P, QUAD, GROUP_VIDEOS], F32, tag="repeated", name="repeated")
                nc.scalar.copy(
                    out=made["repeated"][:],
                    in_=top[:, group_videos(group)].unsqueeze(1).to_broadcast([P, QUAD, GROUP_VIDEOS]),
                )

            def turn(tag, bufs):
                bank = psum.tile([P, P], F32, tag=tag, name="turned_top", bufs=bufs)
                nc.tensor.transpose(
                    bank[:], made["repeated"][:].rearrange("a s b -> a (s b)"), ident_f32[:]
                )
                return lambda: nc.scalar.copy(out=top_turned[:, group, :], in_=bank[:])

            return [plain(repeat), turning(turn)]

        def turn_products(group, tag, bufs):
            bank = psum.tile([P, BLOCKS, P], F32, tag=tag, name="turned_products", bufs=bufs)
            columns = product_sums[group][:].rearrange("a v b -> a (v b)")
            for k in range(BLOCKS):
                nc.tensor.transpose(bank[:, k, :], columns[:, k * P : (k + 1) * P], ident_f32[:])
            return bank

        def turn_product_pieces(group):

            def turn(tag, bufs):
                bank = turn_products(group, tag, bufs)
                return lambda: store(group, 1, unit_blocks(TOKEN_UNIT), bank[:])

            return [turning(turn)]

        def take_logarithms(groups):
            for group in groups:
                weights = sums[group, 0][:, :, :]
                nc.scalar.activation(out=weights, in_=weights, func=FN.Ln)

        def invert_logarithms(group, blocks):
            weights = sums[group, 0][:, blocks, :]
            nc.scalar.activation(out=weights, in_=weights, func=FN.Exp, scale=-1.0)

        def invert_block(block):
            weights = sums[LAST, 0][:, block, :]
            over_tokens = block - TOKEN_UNIT * BLOCKS
            source = weights if over_tokens < 0 else weight_banks[LAST][:, over_tokens, :]
            nc.vector.reciprocal(out=weights, in_=source)

        def weighing_pieces(group, blocks, multiply_engine):
            weights = sums[group, 0][:, blocks, :]
            means = sums[group, 1][:, blocks, :]

            def divide():
                multiply_engine.tensor_tensor(out=means, in0=means, in1=weights, op=ALU.mult)

            def deviate():
                tops = top_turned[:, group, :].unsqueeze(1)
                nc.vector.tensor_tensor(
                    out=means, in0=means,
                    in1=tops.to_broadcast([P, blocks.stop - blocks.start, P]), op=ALU.subtract,
                )

            def weigh_means():
                nc.scalar.activation(out=weights, in_=means, func=FN.Exp, scale=sharp_top[:, 0:1])

            def form_products():
                multiply_engine.tensor_tensor(out=means, in0=means, in1=weights, op=ALU.mult)

            return [plain(divide), plain(deviate), plain(weigh_means), plain(form_products)]

        def adding_pieces(group, units):
            blocks = [block for unit in units for block in range(UNITS * BLOCKS)[unit_blocks(unit)]]

            def turn_back(tag, bufs):
                bank = psum.tile(
                    [P, 2, QUAD, GROUP_VIDEOS], F32, tag=tag, name="turned_back", bufs=bufs
                )
                for plane in range(2):
                    for block in blocks:
                        transpose_add(
                            bank[:, plane, :, :].rearrange("a s b -> a (s b)"),
                            sums[group, plane][:, block, :],
                            block == blocks[0],
                            block == blocks[-1],
                        )
                return lambda: nc.vector.tensor_reduce(
                    out=statistics[:, units[0], :, group_videos(group)],
                    in_=bank[:].rearrange("a q s b -> a q b s"),
                    axis=INNERMOST,
                    op=ALU.add,
                )

            return [turning(turn_back)]

        def result_pieces(groups, halves):
            videos = slice(groups[0] * GROUP_VIDEOS, (groups[-1] + 1) * GROUP_VIDEOS)

            def invert(unit):
                weights = statistics[:, unit, 0, videos]
                nc.vector.reciprocal(out=weights, in_=weights)

            def divide(unit):
                products = statistics[:, unit, 1, videos]
                nc.vector.tensor_tensor(
                    out=products, in0=products, in1=statistics[:, unit, 0, videos], op=ALU.mult
                )

            def add_mean(unit):
                nc.vector.scalar_tensor_tensor(
                    out=result[:, videos], in0=statistics[:, unit, 1, videos],
                    scalar=half_mask_top[:, 0:1], in1=result[:, videos], op0=ALU.mult, op1=ALU.add,
                )

            def join_halves():
                joined = statistics[:, 0, :, videos]
                nc.vector.tensor_tensor(
                    out=joined, in0=joined, in1=statistics[:, 1, :, videos], op=ALU.add
                )

            def invert_both():
                invert(TOKEN_UNIT)
                invert(0)

            def divide_both():
                divide(TOKEN_UNIT)
                divide(0)
                add_mean(TOKEN_UNIT)

            def put_out():
                add_mean(0)
                nc.sync.dma_start(out=out[:, videos], in_=result[:, videos])

            joining = [reading(join_halves)] if halves else []
            return joining + [reading(invert_both), plain(divide_both), plain(put_out)]

        def scale_top_pieces(group):
            videos = group_videos(group)
            return [plain(lambda: nc.vector.tensor_scalar_mul(
                out=result[:, videos], in0=top[:, videos], scalar1=mask_top[:, 0:1]
            ))]

        def woven(chains):
            pieces = []
            for slot in range(len(chains) + max(len(chain) for chain in chains)):
                for number, chain in enumerate(chains):
                    if 0 <= slot - number < len(chain):
                        pieces.append(chain[slot - number])
            return pieces

        queues = ([], [], [])

        def wait_for(number, step, pieces):
            queues[number].extend([(step, piece) for piece in pieces])

        def group_chains(groups):
            chains = []
            for group in groups:
                adding = ([], adding_pieces(group, range(TOKEN_UNIT)), adding_pieces(group, [TOKEN_UNIT]))
                for unit in range(UNITS):
                    blocks = unit_blocks(unit)
                    invert = plain(lambda group=group, blocks=blocks: invert_logarithms(group, blocks))
                    weighing = weighing_pieces(group, blocks, nc.gpsimd)
                    chains.append([invert] + weighing + adding[unit])
            return chains

        for number, groups in enumerate((list(range(LAST - 1)), [LAST - 1])):
            swept = (groups[-1] + 2) * TOKENS
            stored = swept + FRAME_LAG
            wait_for(number, swept, woven([
                turn_top_pieces(group) + scale_top_pieces(group) for group in groups
            ]))
            wait_for(number, swept, woven([turn_product_pieces(group) for group in groups]))
            logarithms = max(stored, LOG_STEP)
            wait_for(number, logarithms, [plain(lambda groups=groups: take_logarithms(groups))])
            wait_for(number, stored, woven(group_chains(groups)))
            wait_for(number, stored, result_pieces(groups, False))

        def quad_stored(quad):
            return FIRST_STEPS + (quad + 1) * QUAD + FRAME_LAG

        wait_for(2, FIRST_STEPS, turn_top_pieces(LAST) + scale_top_pieces(LAST))
        for quad in range(QUADS - 1):
            wait_for(2, quad_stored(quad), [plain(lambda quad=quad: invert_block(quad))])
            if quad == BLOCKS - 1:
                wait_for(2, quad_stored(quad), weighing_pieces(LAST, unit_blocks(0), nc.gpsimd))
                wait_for(2, quad_stored(quad), adding_pieces(LAST, [0]))
        wait_for(
            2, quad_stored(QUADS - 2), weighing_pieces(LAST, slice(BLOCKS, QUADS - 1), nc.gpsimd)
        )

        def finish_last_group(turned_products):
            first_block = TOKEN_UNIT * BLOCKS

            def works(blocks):
                return [work for turns, work in weighing_pieces(LAST, blocks, nc.vector)]

            def divide(first, stop):
                blocks = slice(first_block + first, first_block + stop)
                nc.vector.scalar_tensor_tensor(
                    out=sums[LAST, 1][:, blocks, :], in0=turned_products[:, first:stop, :],
                    scalar=nudge[:, 1:2], in1=sums[LAST, 0][:, blocks, :], op0=ALU.add, op1=ALU.mult,
                )

            deviate_a, weigh_a, form_a = works(slice(first_block, first_block + 2))[1:]
            deviate_b, weigh_b, form_b = works(slice(first_block + 2, first_block + BLOCKS))[1:]
            divide_quad, deviate_quad, weigh_quad, form_quad = works(slice(QUADS - 1, QUADS))
            divide(0, 2)
            invert_block(first_block + 3)
            deviate_a()
            weigh_a()
            divide(2, BLOCKS)
            invert_block(QUADS - 1)
            deviate_b()
            weigh_b()
            form_a()
            divide_quad()
            form_b()
            deviate_quad()
            weigh_quad()
            form_quad()
            added = [
                work("first", 2)
                for unit in (TOKEN_UNIT, 1)
                for turns, work in adding_pieces(LAST, [unit])
            ]
            for reader in added:
                reader()
            for turns, work in result_pieces([LAST], True):
                work()

        readers = []

        def serve(queue, tag, bufs):
            turns, work = queue[0][1]
            queue.remove(queue[0])
            if turns:
                readers.append(work(tag, bufs))
            else:
                work()

        def read_turned():
            for reader in readers:
                reader()
            readers.clear()

        with tc.manual_schedule():
            for step in range(TOKENS, STEPS + FRAME_LAG + 1):
                pipeline_step(step)
                read_turned()
                if step == STEPS + TOKEN_LAG - 1:
                    turned_products = turn_products(LAST, "first", 2)
                    for block in range(TOKEN_UNIT * BLOCKS, UNITS * BLOCKS - 1):
                        invert_block(block)
                sweeping = step < FIRST_STEPS
                tag = "quad_sums%d" % (1 - (step - FRAME_LAG) % QUAD // 2) if sweeping else "first"
                for number, most in enumerate((PIECES_PER_STEP, PIECES_PER_STEP, 1)):
                    queue = queues[number]
                    for turn in range(most):
                        if not queue or queue[0][0] > step:
                            break
                        turns = queue[0][1][0]
                        if turns is None and readers:
                            break
                        if turns and (readers if sweeping or number < 2 else len(readers) > 1):
                            break
                        if turns and sweeping and step % 2 == 1:
                            break
                        serve(queue, tag, 1 if sweeping else 2)
            read_turned()
            for queue in queues:
                while queue:
                    serve(queue, "first", 2)
                    read_turned()
            finish_last_group(turned_products)
